import numpy as np
import ml_dtypes


BF16 = ml_dtypes.bfloat16


def bf(x):
    return np.asarray(x, np.float32).astype(BF16)


def f64(x):
    return np.asarray(x).astype(np.float64)


E2M1 = np.array([0.0, 0.5, 1.0, 1.5, 2.0, 3.0, 4.0, 6.0, -0.0, -0.5, -1.0, -1.5, -2.0, -3.0, -4.0, -6.0])


def pack_weight(w, fmt):
    k, n = w.shape
    w = f64(bf(w)).reshape(k // 32, 32, n)
    amax = np.abs(w).max(1)
    if fmt == "e4m3":
        byte = np.frexp(amax)[1] - 1 + 127 - 7
    else:
        mant, ex = np.frexp(amax / 6.0)
        byte = np.where(mant > 0.5, ex, ex - 1) + 127
    byte = np.clip(np.where(amax > 0, byte, 1), 1, 254)
    scaled = (w * np.exp2(127.0 - byte)[:, None, :]).reshape(k, n).astype(np.float32)
    by_word = np.ascontiguousarray(scaled.reshape(k // 512, 128, 4, n).transpose(0, 1, 3, 2))
    if fmt == "e4m3":
        words = by_word.astype(ml_dtypes.float8_e4m3fn).view(np.uint8)
    else:
        c = by_word.astype(ml_dtypes.float4_e2m1fn).view(np.uint8) & 0xF
        words = c[..., 0::2] | (c[..., 1::2] << 4)
    return np.ascontiguousarray(words), np.ascontiguousarray(byte.astype(np.uint8).reshape(k // 512, 16, n))


def unpack_weight(words, scales, fmt):
    g, p, n, _ = words.shape
    if fmt == "e4m3":
        vals = np.ascontiguousarray(words).view(ml_dtypes.float8_e4m3fn).astype(np.float64)
    else:
        nib = np.empty((g, p, n, 4), np.uint8)
        nib[..., 0::2] = words & 0xF
        nib[..., 1::2] = words >> 4
        vals = E2M1[nib]
    vals = vals * np.repeat(np.exp2(scales.astype(np.float64) - 127.0), 8, axis=1)[..., None]
    return vals.transpose(0, 1, 3, 2).reshape(g * 512, n)

def pack4(w):
    words, scales = pack_weight(w, "e2m1")
    return words.reshape(words.shape[0], 128, -1), scales


def unpack4(words, scales):
    return unpack_weight(words.reshape(words.shape[0], 128, -1, 2), scales, "e2m1")


def kspread(k):
    return np.exp2(np.repeat(np.random.randint(-6, 7, k // 32), 32).astype(np.float64))


B, N, DIM, H, DH = 2, 1024, 2048, 16, 96
D1 = DH // 3


def rotate_half(t):
    d = t.shape[-1]
    t1, t2 = t[..., : (d + 1) // 2], t[..., (d + 1) // 2:]
    return np.concatenate((-t2, t1), axis=-1)


def apply_rope(t, freqs):
    return t * np.cos(freqs) + rotate_half(t) * np.sin(freqs)


def rope3(t, fs):
    return np.concatenate([apply_rope(ts, f) for ts, f in zip(np.split(t, (D1, 2 * D1), axis=-1), fs)], axis=-1)


def setup_inputs():
    s = kspread(DIM)
    x = np.random.standard_normal((B, N, DIM)) * s
    x_words, x_scales = pack4(x.reshape(B * N, DIM).T)
    f1 = bf(np.random.uniform(0.0, 1.0, (N, D1)))
    f2 = bf(np.random.uniform(0.0, 1.0, (N, D1)))
    f3 = bf(np.random.uniform(0.0, 1.0, (N, D1)))
    words, scales = pack4(np.random.standard_normal((DIM, 3 * H * DH)) / np.sqrt(DIM) / s[:, None])
    return {"x_words": x_words, "x_scales": x_scales, "f1": f1, "f2": f2, "f3": f3, "Wqkv_words": words, "Wqkv_scales": scales}


def reference(x_words, x_scales, f1, f2, f3, Wqkv_words, Wqkv_scales):
    qkv = unpack4(x_words, x_scales).T.reshape(B, N, DIM) @ unpack4(Wqkv_words, Wqkv_scales)
    q, k, v = np.split(qkv, 3, axis=-1)
    to_heads = lambda t: t.reshape(B, N, H, DH).transpose(0, 2, 1, 3)
    q, k, v = to_heads(q), to_heads(k), to_heads(v)
    fs = (f64(f1), f64(f2), f64(f3))
    return rope3(q, fs), rope3(k, fs), v

@@ -1,0 +1,230 @@
+from contextlib import ExitStack
+
+import concourse.mybir as mybir
+
+F32 = mybir.dt.float32
+BF16 = mybir.dt.bfloat16
+U8 = mybir.dt.uint8
+I32 = mybir.dt.int32
+FP4X4 = mybir.dt.float4_e2m1fn_x4
+ACT = mybir.ActivationFunctionType
+ALU = mybir.AluOpType
+
+P = 128
+G = 4
+TOK = 4
+CHUNK = P * TOK
+NCHUNK = 4
+HEADS = 16
+DH = 96
+PART = HEADS * DH
+BANK = 512
+NB = PART // BANK
+GRP = 32
+HALF = GRP // 2
+REP = 6
+TABW = REP * DH
+
+FLOPS = 2 * 2048 * 2048 * 4608
+
+
+def tile_attention_pa_kernel(
+    tc, x_words, x_scales, f1, f2, f3, Wqkv_words, Wqkv_scales, out_0, out_1, out_2
+):
+    nc = tc.nc
+    outs = (out_0, out_1, out_2)
+
+    with ExitStack() as ctx:
+        keep = ctx.enter_context(tc.tile_pool(name="keep", bufs=1))
+        xperm = ctx.enter_context(tc.tile_pool(name="xperm", bufs=2))
+        prod = ctx.enter_context(tc.tile_pool(name="prod", bufs=3))
+        stages = ctx.enter_context(tc.tile_pool(name="stages", bufs=3))
+        psum = ctx.enter_context(tc.psum_pool(name="psum", bufs=8))
+
+        w_codes = [
+            keep.tile([P, G, 2 * BANK], U8, name="w_codes%d" % k, align_bytes=64) for k in range(3 * NB)
+        ]
+        w_planes = [keep.tile([P, G, PART], U8, name="w_planes%d" % k, align_bytes=64) for k in range(3)]
+        xr_codes = [keep.tile([P, G, 2 * CHUNK], U8, name="xr_codes%d" % k, align_bytes=64) for k in range(2)]
+        xr_planes = [keep.tile([P, G, CHUNK], U8, name="xr_planes%d" % k, align_bytes=64) for k in range(2)]
+
+        def load_scale_rows(planes, scales):
+            for q in range(4):
+                nc.sync.dma_start(
+                    out=planes[32 * q : 32 * q + 4, :, :].bitcast(I32),
+                    in_=scales[:, 4 * q : 4 * q + 4, :].rearrange("g r n -> r g n").bitcast(I32),
+                )
+
+        def load_x_codes(c):
+            nc.sync.dma_start(
+                out=xr_codes[c % 2][:].bitcast(I32),
+                in_=x_words[:, :, 2 * CHUNK * c : 2 * CHUNK * (c + 1)].rearrange("g p n -> p g n").bitcast(I32),
+            )
+
+        def load_x_scales(c):
+            load_scale_rows(xr_planes[c % 2], x_scales[:, :, CHUNK * c : CHUNK * (c + 1)])
+
+        def load_w_codes(k):
+            nc.sync.dma_start(
+                out=w_codes[k][:].bitcast(I32),
+                in_=Wqkv_words[:, :, 2 * BANK * k : 2 * BANK * (k + 1)].rearrange("g p n -> p g n").bitcast(I32),
+            )
+
+        def load_w_scales(part):
+            load_scale_rows(w_planes[part], Wqkv_scales[:, :, PART * part : PART * (part + 1)])
+
+        warm = keep.tile([P, 1], F32, name="warm")
+        warm2 = keep.tile([P, 1], F32, name="warm2")
+        nc.gpsimd.memset(warm[:], 0.0)
+        nc.scalar.activation(out=warm2[:], in_=warm[:], func=ACT.Sin)
+
+        nc.vector.memset(xr_planes[0][:].bitcast(I32), 0)
+        nc.vector.memset(w_planes[0][:].bitcast(I32), 0)
+        nc.vector.memset(xr_planes[1][:].bitcast(I32), 0)
+        nc.vector.memset(w_planes[1][:].bitcast(I32), 0)
+        nc.vector.memset(w_planes[2][:].bitcast(I32), 0)
+
+        fraw = keep.tile([P, 3, 2, TOK, GRP], BF16, name="fraw")
+        for i, f in enumerate((f1, f2, f3)):
+            nc.scalar.dma_start(
+                out=fraw[:, i].rearrange("p c t j -> p c (t j)"),
+                in_=f.rearrange("(c p t) j -> p c (t j)", c=2, t=TOK),
+            )
+
+        load_x_codes(0)
+        load_x_scales(0)
+        load_w_scales(0)
+        for k in range(NB):
+            load_w_codes(k)
+        load_x_scales(1)
+        load_w_scales(1)
+        load_x_codes(1)
+        for k in range(NB, 2 * NB):
+            load_w_codes(k)
+        load_w_scales(2)
+        for k in range(2 * NB, 3 * NB):
+            load_w_codes(k)
+
+        half = keep.tile([P, 3, 2, TOK, GRP], F32, name="half")
+        sq = keep.tile([P, 3, 2, TOK, GRP], F32, name="sq")
+        nc.scalar.activation(
+            out=half[:].rearrange("p i c t j -> p (i c t j)"),
+            in_=fraw[:].rearrange("p i c t j -> p (i c t j)"),
+            func=ACT.Sin,
+            scale=0.5,
+        )
+        nc.scalar.activation(
+            out=sq[:].rearrange("p i c t j -> p (i c t j)"),
+            in_=half[:].rearrange("p i c t j -> p (i c t j)"),
+            func=ACT.Square,
+        )
+        cos_tab = {}
+        sin_tab = {}
+        for cc in range(2):
+            for t in range(TOK):
+                ct = keep.tile([P, TABW], F32, name="cos%d_%d" % (cc, t))
+                nc.scalar.activation(
+                    out=ct[:].rearrange("p (r i j) -> p r i j", i=3, j=GRP),
+                    in_=sq[:, :, cc, t, :].unsqueeze(1).to_broadcast([P, REP, 3, GRP]),
+                    func=ACT.Copy,
+                    scale=-2.0,
+                    bias=1.0,
+                )
+                st = keep.tile([P, TABW], F32, name="sin%d_%d" % (cc, t))
+                sv = st[:].rearrange("p (r i h j) -> p r i h j", i=3, h=2, j=HALF)
+                for h, sign in ((0, -1.0), (1, 1.0)):
+                    nc.scalar.activation(
+                        out=sv[:, :, :, h, :],
+                        in_=fraw[:, :, cc, t, HALF * h : HALF * (h + 1)].unsqueeze(1).to_broadcast([P, REP, 3, HALF]),
+                        func=ACT.Sin,
+                        scale=sign,
+                    )
+                cos_tab[(cc, t)] = ct
+                sin_tab[(cc, t)] = st
+
+        def permute(c, t):
+            xc = xperm.tile([P, G, 2 * P], U8, name="xc%d" % t, tag="xc%d" % t, align_bytes=64)
+            nc.vector.tensor_copy(
+                out=xc[:].rearrange("p g (m b) -> p g m b", b=2),
+                in_=xr_codes[c % 2][:].rearrange("p g (m t b) -> p t g m b", t=TOK, b=2)[:, t],
+            )
+            xs = xperm.tile([P, G, P], U8, name="xs%d" % t, tag="xs%d" % t, align_bytes=64)
+            nc.vector.tensor_copy(
+                out=xs[:],
+                in_=xr_planes[c % 2][:].rearrange("p g (m t) -> p t g m", t=TOK)[:, t],
+            )
+            return xc, xs
+
+        x_now = [permute(0, t) for t in range(TOK)]
+        load_x_codes(2)
+        load_x_scales(2)
+
+        for c in range(NCHUNK):
+            b, cc = divmod(c, 2)
+            x_next = []
+            for part in range(3):
+                stage = stages.tile([P, HEADS, TOK, DH], F32, name="stage", tag="stage")
+                for t in range(TOK):
+                    xc, xs = x_now[t]
+                    accs = []
+                    for i in range(NB):
+                        acc = psum.tile([P, BANK], F32, name="acc", tag="acc")
+                        for g in range(G):
+                            nc.tensor.matmul_mx(
+                                out=acc[:],
+                                lhsT=xc[:, g, :].bitcast(FP4X4),
+                                lhsT_scale=xs[:, g, :],
+                                rhs=w_codes[NB * part + i][:, g, :].bitcast(FP4X4),
+                                rhs_scale=w_planes[part][:, g, BANK * i : BANK * (i + 1)],
+                                start=(g == 0),
+                                stop=(g == G - 1),
+                            )
+                        accs.append(acc)
+                    if part < 2:
+                        t1 = prod.tile([P, PART], F32, name="t1", tag="t1")
+                        t2 = prod.tile([P, PART], F32, name="t2", tag="t2")
+                        for i in range(NB):
+                            cols = slice(BANK * i, BANK * (i + 1))
+                            tab = slice(GRP * i, GRP * i + BANK)
+                            nc.vector.tensor_tensor(
+                                out=t1[:, cols], in0=accs[i][:], in1=cos_tab[(cc, t)][:, tab], op=ALU.mult
+                            )
+                            u = accs[i][:].rearrange("p (a h j) -> p a h j", h=2, j=HALF)
+                            t2v = t2[:, cols].rearrange("p (a h j) -> p a h j", h=2, j=HALF)
+                            sv = sin_tab[(cc, t)][:, tab].rearrange("p (a h j) -> p a h j", h=2, j=HALF)
+                            for h in range(2):
+                                nc.vector.tensor_tensor(
+                                    out=t2v[:, :, h, :], in0=u[:, :, 1 - h, :], in1=sv[:, :, h, :], op=ALU.mult
+                                )
+                        nc.gpsimd.tensor_tensor(
+                            out=stage[:, :, t, :],
+                            in0=t1[:].rearrange("p (h d) -> p h d", d=DH),
+                            in1=t2[:].rearrange("p (h d) -> p h d", d=DH),
+                            op=ALU.add,
+                        )
+                    else:
+                        for i in range(NB):
+                            c0 = BANK * i
+                            lead = (-c0) % DH
+                            whole = (BANK - lead) // DH
+                            tail = BANK - lead - whole * DH
+                            if lead:
+                                nc.scalar.copy(out=stage[:, c0 // DH, t, DH - lead :], in_=accs[i][:, :lead])
+                            h0 = (c0 + lead) // DH
+                            nc.scalar.copy(
+                                out=stage[:, h0 : h0 + whole, t, :],
+                                in_=accs[i][:, lead : lead + whole * DH].rearrange("p (h d) -> p h d", d=DH),
+                            )
+                            if tail:
+                                nc.scalar.copy(out=stage[:, h0 + whole, t, :tail], in_=accs[i][:, BANK - tail :])
+                        if c + 1 < NCHUNK:
+                            x_next.append(permute(c + 1, t))
+                eng = nc.sync if part < 2 else nc.scalar
+                eng.dma_start(
+                    out=outs[part][b, :, CHUNK * cc : CHUNK * (cc + 1), :].rearrange("h (p t) d -> p h (t d)", t=TOK),
+                    in_=stage[:].rearrange("p h t d -> p h (t d)"),
+                )
+            if c + 3 < NCHUNK:
+                load_x_codes(c + 3)
+                load_x_scales(c + 3)
+            x_now = x_next

@@ -24,6 +24,7 @@ GRP = 32
 HALF = GRP // 2
 REP = 6
 TABW = REP * DH
+FIRST_HEAD = [0, 5, 10, 16]
 
 FLOPS = 2 * 2048 * 2048 * 4608
 
@@ -38,13 +39,13 @@ def tile_attention_pa_kernel(
         keep = ctx.enter_context(tc.tile_pool(name="keep", bufs=1))
         xperm = ctx.enter_context(tc.tile_pool(name="xperm", bufs=2))
         prod = ctx.enter_context(tc.tile_pool(name="prod", bufs=3))
-        stages = ctx.enter_context(tc.tile_pool(name="stages", bufs=3))
+        stages = ctx.enter_context(tc.tile_pool(name="stages", bufs=2))
         psum = ctx.enter_context(tc.psum_pool(name="psum", bufs=8))
 
         w_codes = [
             keep.tile([P, G, 2 * BANK], U8, name="w_codes%d" % k, align_bytes=64) for k in range(3 * NB)
         ]
-        w_planes = [keep.tile([P, G, PART], U8, name="w_planes%d" % k, align_bytes=64) for k in range(3)]
+        w_planes = [keep.tile([P, G, BANK], U8, name="w_planes%d" % k, align_bytes=64) for k in range(3 * NB)]
         xr_codes = [keep.tile([P, G, 2 * CHUNK], U8, name="xr_codes%d" % k, align_bytes=64) for k in range(2)]
         xr_planes = [keep.tile([P, G, CHUNK], U8, name="xr_planes%d" % k, align_bytes=64) for k in range(2)]
 
@@ -70,40 +71,51 @@ def tile_attention_pa_kernel(
                 in_=Wqkv_words[:, :, 2 * BANK * k : 2 * BANK * (k + 1)].rearrange("g p n -> p g n").bitcast(I32),
             )
 
-        def load_w_scales(part):
-            load_scale_rows(w_planes[part], Wqkv_scales[:, :, PART * part : PART * (part + 1)])
+        def load_w_scales(k):
+            load_scale_rows(w_planes[k], Wqkv_scales[:, :, BANK * k : BANK * (k + 1)])
+
+        def permute(c, t):
+            xc = xperm.tile([P, G, 2 * P], U8, name="xc%d" % t, tag="xc%d" % t, align_bytes=64)
+            nc.vector.tensor_copy(
+                out=xc[:].rearrange("p g (m b) -> p g m b", b=2),
+                in_=xr_codes[c % 2][:].rearrange("p g (m t b) -> p t g m b", t=TOK, b=2)[:, t],
+            )
+            xs = xperm.tile([P, G, P], U8, name="xs%d" % t, tag="xs%d" % t, align_bytes=64)
+            nc.vector.tensor_copy(
+                out=xs[:],
+                in_=xr_planes[c % 2][:].rearrange("p g (m t) -> p t g m", t=TOK)[:, t],
+            )
+            return xc, xs
 
         warm = keep.tile([P, 1], F32, name="warm")
         warm2 = keep.tile([P, 1], F32, name="warm2")
         nc.gpsimd.memset(warm[:], 0.0)
         nc.scalar.activation(out=warm2[:], in_=warm[:], func=ACT.Sin)
 
-        nc.vector.memset(xr_planes[0][:].bitcast(I32), 0)
-        nc.vector.memset(w_planes[0][:].bitcast(I32), 0)
-        nc.vector.memset(xr_planes[1][:].bitcast(I32), 0)
-        nc.vector.memset(w_planes[1][:].bitcast(I32), 0)
-        nc.vector.memset(w_planes[2][:].bitcast(I32), 0)
-
         fraw = keep.tile([P, 3, 2, TOK, GRP], BF16, name="fraw")
         for i, f in enumerate((f1, f2, f3)):
-            nc.scalar.dma_start(
+            nc.gpsimd.dma_start(
                 out=fraw[:, i].rearrange("p c t j -> p c (t j)"),
                 in_=f.rearrange("(c p t) j -> p c (t j)", c=2, t=TOK),
             )
 
+        nc.vector.memset(xr_planes[0][:].bitcast(I32), 0)
+        nc.vector.memset(w_planes[0][:].bitcast(I32), 0)
         load_x_codes(0)
+        load_w_codes(0)
         load_x_scales(0)
         load_w_scales(0)
-        for k in range(NB):
+        x_now = [permute(0, t) for t in range(TOK)]
+        for k in range(1, 3 * NB):
+            nc.vector.memset(w_planes[k][:].bitcast(I32), 0)
+            load_w_scales(k)
             load_w_codes(k)
-        load_x_scales(1)
-        load_w_scales(1)
-        load_x_codes(1)
-        for k in range(NB, 2 * NB):
-            load_w_codes(k)
-        load_w_scales(2)
-        for k in range(2 * NB, 3 * NB):
-            load_w_codes(k)
+            if k == 2:
+                nc.vector.memset(xr_planes[1][:].bitcast(I32), 0)
+                load_x_scales(1)
+                load_x_codes(1)
+        load_x_scales(2)
+        load_x_codes(2)
 
         half = keep.tile([P, 3, 2, TOK, GRP], F32, name="half")
         sq = keep.tile([P, 3, 2, TOK, GRP], F32, name="sq")
@@ -142,32 +154,41 @@ def tile_attention_pa_kernel(
                 cos_tab[(cc, t)] = ct
                 sin_tab[(cc, t)] = st
 
-        def permute(c, t):
-            xc = xperm.tile([P, G, 2 * P], U8, name="xc%d" % t, tag="xc%d" % t, align_bytes=64)
-            nc.vector.tensor_copy(
-                out=xc[:].rearrange("p g (m b) -> p g m b", b=2),
-                in_=xr_codes[c % 2][:].rearrange("p g (m t b) -> p t g m b", t=TOK, b=2)[:, t],
-            )
-            xs = xperm.tile([P, G, P], U8, name="xs%d" % t, tag="xs%d" % t, align_bytes=64)
-            nc.vector.tensor_copy(
-                out=xs[:],
-                in_=xr_planes[c % 2][:].rearrange("p g (m t) -> p t g m", t=TOK)[:, t],
-            )
-            return xc, xs
+        def pieces(i):
+            c0 = BANK * i
+            lead = (-c0) % DH
+            whole = (BANK - lead) // DH
+            tail = BANK - lead - whole * DH
+            runs = []
+            if lead:
+                runs.append((0, lead, c0 // DH, DH - lead))
+            runs.append((lead, whole * DH, (c0 + lead) // DH, 0))
+            if tail:
+                runs.append((BANK - tail, tail, (c0 + lead) // DH + whole, 0))
+            return runs
 
-        x_now = [permute(0, t) for t in range(TOK)]
-        load_x_codes(2)
-        load_x_scales(2)
+        def stage_view(stage, head, n_heads):
+            j = max(k for k in range(NB) if FIRST_HEAD[k] <= head)
+            return stage[j][:, head - FIRST_HEAD[j] : head - FIRST_HEAD[j] + n_heads]
 
         for c in range(NCHUNK):
             b, cc = divmod(c, 2)
             x_next = []
             for part in range(3):
-                stage = stages.tile([P, HEADS, TOK, DH], F32, name="stage", tag="stage")
-                for t in range(TOK):
-                    xc, xs = x_now[t]
-                    accs = []
-                    for i in range(NB):
+                stage = [
+                    stages.tile([P, FIRST_HEAD[j + 1] - FIRST_HEAD[j], TOK, DH], F32, name="stage%d" % j, tag="stage%d" % j)
+                    for j in range(NB)
+                ]
+                dst = outs[part][b, :, CHUNK * cc : CHUNK * (cc + 1), :]
+                eng = nc.sync if part < 2 else nc.scalar
+                for i in range(NB):
+                    last = c == NCHUNK - 1 and part == 2 and i == NB - 1
+                    heads = slice(FIRST_HEAD[i], FIRST_HEAD[i + 1])
+                    if part < 2:
+                        t1 = prod.tile([P, TOK, BANK], F32, name="t1", tag="t1")
+                        t2 = prod.tile([P, TOK, BANK], F32, name="t2", tag="t2")
+                    for t in range(TOK):
+                        xc, xs = x_now[t]
                         acc = psum.tile([P, BANK], F32, name="acc", tag="acc")
                         for g in range(G):
                             nc.tensor.matmul_mx(
@@ -175,56 +196,62 @@ def tile_attention_pa_kernel(
                                 lhsT=xc[:, g, :].bitcast(FP4X4),
                                 lhsT_scale=xs[:, g, :],
                                 rhs=w_codes[NB * part + i][:, g, :].bitcast(FP4X4),
-                                rhs_scale=w_planes[part][:, g, BANK * i : BANK * (i + 1)],
+                                rhs_scale=w_planes[NB * part + i][:, g, :],
                                 start=(g == 0),
                                 stop=(g == G - 1),
                             )
-                        accs.append(acc)
-                    if part < 2:
-                        t1 = prod.tile([P, PART], F32, name="t1", tag="t1")
-                        t2 = prod.tile([P, PART], F32, name="t2", tag="t2")
-                        for i in range(NB):
-                            cols = slice(BANK * i, BANK * (i + 1))
+                        if part < 2:
                             tab = slice(GRP * i, GRP * i + BANK)
                             nc.vector.tensor_tensor(
-                                out=t1[:, cols], in0=accs[i][:], in1=cos_tab[(cc, t)][:, tab], op=ALU.mult
+                                out=t1[:, t, :], in0=acc[:], in1=cos_tab[(cc, t)][:, tab], op=ALU.mult
                             )
-                            u = accs[i][:].rearrange("p (a h j) -> p a h j", h=2, j=HALF)
-                            t2v = t2[:, cols].rearrange("p (a h j) -> p a h j", h=2, j=HALF)
+                            u = acc[:].rearrange("p (a h j) -> p a h j", h=2, j=HALF)
+                            t2v = t2[:, t, :].rearrange("p (a h j) -> p a h j", h=2, j=HALF)
                             sv = sin_tab[(cc, t)][:, tab].rearrange("p (a h j) -> p a h j", h=2, j=HALF)
                             for h in range(2):
                                 nc.vector.tensor_tensor(
                                     out=t2v[:, :, h, :], in0=u[:, :, 1 - h, :], in1=sv[:, :, h, :], op=ALU.mult
                                 )
-                        nc.gpsimd.tensor_tensor(
-                            out=stage[:, :, t, :],
-                            in0=t1[:].rearrange("p (h d) -> p h d", d=DH),
-                            in1=t2[:].rearrange("p (h d) -> p h d", d=DH),
-                            op=ALU.add,
+                        else:
+                            for a, n, head, d in pieces(i):
+                                if n > DH:
+                                    nc.scalar.copy(
+                                        out=stage_view(stage, head, n // DH)[:, :, t, :],
+                                        in_=acc[:, a : a + n].rearrange("p (h d) -> p h d", d=DH),
+                                    )
+                                else:
+                                    nc.scalar.copy(
+                                        out=stage_view(stage, head, 1)[:, 0, t, d : d + n], in_=acc[:, a : a + n]
+                                    )
+                            if i == 0 and c + 1 < NCHUNK:
+                                x_next.append(permute(c + 1, t))
+                            if last:
+                                eng.dma_start(
+                                    out=dst[heads].rearrange("h (p t) d -> p h t d", t=TOK)[:, :, t, :],
+                                    in_=stage[i][:, :, t, :],
+                                )
+                    if part < 2:
+                        for a, n, head, d in pieces(i):
+                            if n > DH:
+                                nc.gpsimd.tensor_tensor(
+                                    out=stage_view(stage, head, n // DH),
+                                    in0=t1[:, :, a : a + n].rearrange("p t (h d) -> p h t d", d=DH),
+                                    in1=t2[:, :, a : a + n].rearrange("p t (h d) -> p h t d", d=DH),
+                                    op=ALU.add,
+                                )
+                            else:
+                                nc.gpsimd.tensor_tensor(
+                                    out=stage_view(stage, head, 1)[:, 0, :, d : d + n],
+                                    in0=t1[:, :, a : a + n],
+                                    in1=t2[:, :, a : a + n],
+                                    op=ALU.add,
+                                )
+                    if not last:
+                        eng.dma_start(
+                            out=dst[heads].rearrange("h (p t) d -> p h (t d)", t=TOK),
+                            in_=stage[i][:].rearrange("p h t d -> p h (t d)"),
                         )
-                    else:
-                        for i in range(NB):
-                            c0 = BANK * i
-                            lead = (-c0) % DH
-                            whole = (BANK - lead) // DH
-                            tail = BANK - lead - whole * DH
-                            if lead:
-                                nc.scalar.copy(out=stage[:, c0 // DH, t, DH - lead :], in_=accs[i][:, :lead])
-                            h0 = (c0 + lead) // DH
-                            nc.scalar.copy(
-                                out=stage[:, h0 : h0 + whole, t, :],
-                                in_=accs[i][:, lead : lead + whole * DH].rearrange("p (h d) -> p h d", d=DH),
-                            )
-                            if tail:
-                                nc.scalar.copy(out=stage[:, h0 + whole, t, :tail], in_=accs[i][:, BANK - tail :])
-                        if c + 1 < NCHUNK:
-                            x_next.append(permute(c + 1, t))
-                eng = nc.sync if part < 2 else nc.scalar
-                eng.dma_start(
-                    out=outs[part][b, :, CHUNK * cc : CHUNK * (cc + 1), :].rearrange("h (p t) d -> p h (t d)", t=TOK),
-                    in_=stage[:].rearrange("p h t d -> p h (t d)"),
-                )
             if c + 3 < NCHUNK:
-                load_x_codes(c + 3)
                 load_x_scales(c + 3)
+                load_x_codes(c + 3)
             x_now = x_next

@@ -41,99 +41,110 @@ def tile_attention_pa_kernel(
         prod = ctx.enter_context(tc.tile_pool(name="prod", bufs=3))
         stages = ctx.enter_context(tc.tile_pool(name="stages", bufs=2))
         psum = ctx.enter_context(tc.psum_pool(name="psum", bufs=8))
+        with tc.manual_schedule():
 
-        w_codes = [
-            keep.tile([P, G, 2 * BANK], U8, name="w_codes%d" % k, align_bytes=64) for k in range(3 * NB)
-        ]
-        w_planes = [keep.tile([P, G, BANK], U8, name="w_planes%d" % k, align_bytes=64) for k in range(3 * NB)]
-        xr_codes = [keep.tile([P, G, 2 * CHUNK], U8, name="xr_codes%d" % k, align_bytes=64) for k in range(2)]
-        xr_planes = [keep.tile([P, G, CHUNK], U8, name="xr_planes%d" % k, align_bytes=64) for k in range(2)]
+            w_codes = [
+                keep.tile([P, G, 2 * BANK], U8, name="w_codes%d" % k, align_bytes=64) for k in range(3 * NB)
+            ]
+            w_planes = [keep.tile([P, G, BANK], U8, name="w_planes%d" % k, align_bytes=64) for k in range(3 * NB)]
+            xr_codes = [keep.tile([P, G, 2 * CHUNK], U8, name="xr_codes%d" % k, align_bytes=64) for k in range(2)]
+            xr_planes = [keep.tile([P, G, CHUNK], U8, name="xr_planes%d" % k, align_bytes=64) for k in range(2)]
 
-        def load_scale_rows(planes, scales):
-            for q in range(4):
+            def load_scale_rows(planes, scales):
+                for q in range(4):
+                    nc.sync.dma_start(
+                        out=planes[32 * q : 32 * q + 4, :, :].bitcast(I32),
+                        in_=scales[:, 4 * q : 4 * q + 4, :].rearrange("g r n -> r g n").bitcast(I32),
+                    )
+
+            def load_x_codes(c):
                 nc.sync.dma_start(
-                    out=planes[32 * q : 32 * q + 4, :, :].bitcast(I32),
-                    in_=scales[:, 4 * q : 4 * q + 4, :].rearrange("g r n -> r g n").bitcast(I32),
+                    out=xr_codes[c % 2][:].bitcast(I32),
+                    in_=x_words[:, :, 2 * CHUNK * c : 2 * CHUNK * (c + 1)].rearrange("g p n -> p g n").bitcast(I32),
                 )
 
-        def load_x_codes(c):
-            nc.sync.dma_start(
-                out=xr_codes[c % 2][:].bitcast(I32),
-                in_=x_words[:, :, 2 * CHUNK * c : 2 * CHUNK * (c + 1)].rearrange("g p n -> p g n").bitcast(I32),
+            def load_x_scales(c):
+                load_scale_rows(xr_planes[c % 2], x_scales[:, :, CHUNK * c : CHUNK * (c + 1)])
+
+            def load_w_codes(k):
+                nc.sync.dma_start(
+                    out=w_codes[k][:].bitcast(I32),
+                    in_=Wqkv_words[:, :, 2 * BANK * k : 2 * BANK * (k + 1)].rearrange("g p n -> p g n").bitcast(I32),
+                )
+
+            def load_w_scales(k):
+                load_scale_rows(w_planes[k], Wqkv_scales[:, :, BANK * k : BANK * (k + 1)])
+
+            def permute(c, t):
+                xc = xperm.tile([P, G, 2 * P], U8, name="xc%d" % t, tag="xc%d" % t, align_bytes=64)
+                nc.vector.tensor_copy(
+                    out=xc[:].rearrange("p g (m b) -> p g m b", b=2),
+                    in_=xr_codes[c % 2][:].rearrange("p g (m t b) -> p t g m b", t=TOK, b=2)[:, t],
+                )
+                xs = xperm.tile([P, G, P], U8, name="xs%d" % t, tag="xs%d" % t, align_bytes=64)
+                nc.vector.tensor_copy(
+                    out=xs[:],
+                    in_=xr_planes[c % 2][:].rearrange("p g (m t) -> p t g m", t=TOK)[:, t],
+                )
+                return xc, xs
+
+            def jobs_of(c):
+                rope = [(part, i) for part in (0, 1) for i in range(NB)]
+                pairs = [rope[2 * j : 2 * j + 2] for j in range(NB)]
+                vals = [[(2, j)] for j in range(NB)]
+                if c == 0:
+                    groups = [vals[0], pairs[0], vals[1], pairs[1], vals[2], pairs[2]]
+                elif c == NCHUNK - 1:
+                    groups = pairs + vals
+                else:
+                    groups = [pairs[0], vals[0], pairs[1], vals[1], pairs[2], vals[2]]
+                return [job for group in groups for job in group]
+
+            warm = keep.tile([P, 1], F32, name="warm")
+            warm2 = keep.tile([P, 1], F32, name="warm2")
+            nc.gpsimd.memset(warm[:], 0.0)
+            nc.scalar.activation(out=warm2[:], in_=warm[:], func=ACT.Sin)
+
+            fraw = keep.tile([P, 3, 2, TOK, GRP], BF16, name="fraw")
+            for i, f in enumerate((f1, f2, f3)):
+                nc.gpsimd.dma_start(
+                    out=fraw[:, i].rearrange("p c t j -> p c (t j)"),
+                    in_=f.rearrange("(c p t) j -> p c (t j)", c=2, t=TOK),
+                )
+
+            first = [NB * part + i for part, i in jobs_of(0)]
+            nc.vector.memset(xr_planes[0][:].bitcast(I32), 0)
+            for k in first:
+                nc.vector.memset(w_planes[k][:].bitcast(I32), 0)
+            nc.vector.memset(xr_planes[1][:].bitcast(I32), 0)
+            load_x_codes(0)
+            load_w_codes(first[0])
+            load_x_scales(0)
+            load_w_scales(first[0])
+            for n, k in enumerate(first[1:]):
+                load_w_scales(k)
+                load_w_codes(k)
+                if n == 1:
+                    load_x_scales(1)
+                    load_x_codes(1)
+
+            half = keep.tile([P, 3, 2, TOK, GRP], F32, name="half")
+            sq = keep.tile([P, 3, 2, TOK, GRP], F32, name="sq")
+            nc.scalar.activation(
+                out=half[:].rearrange("p i c t j -> p (i c t j)"),
+                in_=fraw[:].rearrange("p i c t j -> p (i c t j)"),
+                func=ACT.Sin,
+                scale=0.5,
             )
-
-        def load_x_scales(c):
-            load_scale_rows(xr_planes[c % 2], x_scales[:, :, CHUNK * c : CHUNK * (c + 1)])
-
-        def load_w_codes(k):
-            nc.sync.dma_start(
-                out=w_codes[k][:].bitcast(I32),
-                in_=Wqkv_words[:, :, 2 * BANK * k : 2 * BANK * (k + 1)].rearrange("g p n -> p g n").bitcast(I32),
+            nc.scalar.activation(
+                out=sq[:].rearrange("p i c t j -> p (i c t j)"),
+                in_=half[:].rearrange("p i c t j -> p (i c t j)"),
+                func=ACT.Square,
             )
+            cos_tab = {}
+            sin_tab = {}
 
-        def load_w_scales(k):
-            load_scale_rows(w_planes[k], Wqkv_scales[:, :, BANK * k : BANK * (k + 1)])
-
-        def permute(c, t):
-            xc = xperm.tile([P, G, 2 * P], U8, name="xc%d" % t, tag="xc%d" % t, align_bytes=64)
-            nc.vector.tensor_copy(
-                out=xc[:].rearrange("p g (m b) -> p g m b", b=2),
-                in_=xr_codes[c % 2][:].rearrange("p g (m t b) -> p t g m b", t=TOK, b=2)[:, t],
-            )
-            xs = xperm.tile([P, G, P], U8, name="xs%d" % t, tag="xs%d" % t, align_bytes=64)
-            nc.vector.tensor_copy(
-                out=xs[:],
-                in_=xr_planes[c % 2][:].rearrange("p g (m t) -> p t g m", t=TOK)[:, t],
-            )
-            return xc, xs
-
-        warm = keep.tile([P, 1], F32, name="warm")
-        warm2 = keep.tile([P, 1], F32, name="warm2")
-        nc.gpsimd.memset(warm[:], 0.0)
-        nc.scalar.activation(out=warm2[:], in_=warm[:], func=ACT.Sin)
-
-        fraw = keep.tile([P, 3, 2, TOK, GRP], BF16, name="fraw")
-        for i, f in enumerate((f1, f2, f3)):
-            nc.gpsimd.dma_start(
-                out=fraw[:, i].rearrange("p c t j -> p c (t j)"),
-                in_=f.rearrange("(c p t) j -> p c (t j)", c=2, t=TOK),
-            )
-
-        nc.vector.memset(xr_planes[0][:].bitcast(I32), 0)
-        nc.vector.memset(w_planes[0][:].bitcast(I32), 0)
-        load_x_codes(0)
-        load_w_codes(0)
-        load_x_scales(0)
-        load_w_scales(0)
-        x_now = [permute(0, t) for t in range(TOK)]
-        for k in range(1, 3 * NB):
-            nc.vector.memset(w_planes[k][:].bitcast(I32), 0)
-            load_w_scales(k)
-            load_w_codes(k)
-            if k == 2:
-                nc.vector.memset(xr_planes[1][:].bitcast(I32), 0)
-                load_x_scales(1)
-                load_x_codes(1)
-        load_x_scales(2)
-        load_x_codes(2)
-
-        half = keep.tile([P, 3, 2, TOK, GRP], F32, name="half")
-        sq = keep.tile([P, 3, 2, TOK, GRP], F32, name="sq")
-        nc.scalar.activation(
-            out=half[:].rearrange("p i c t j -> p (i c t j)"),
-            in_=fraw[:].rearrange("p i c t j -> p (i c t j)"),
-            func=ACT.Sin,
-            scale=0.5,
-        )
-        nc.scalar.activation(
-            out=sq[:].rearrange("p i c t j -> p (i c t j)"),
-            in_=half[:].rearrange("p i c t j -> p (i c t j)"),
-            func=ACT.Square,
-        )
-        cos_tab = {}
-        sin_tab = {}
-        for cc in range(2):
-            for t in range(TOK):
+            def build_tables(cc, t):
                 ct = keep.tile([P, TABW], F32, name="cos%d_%d" % (cc, t))
                 nc.scalar.activation(
                     out=ct[:].rearrange("p (r i j) -> p r i j", i=3, j=GRP),
@@ -154,104 +165,118 @@ def tile_attention_pa_kernel(
                 cos_tab[(cc, t)] = ct
                 sin_tab[(cc, t)] = st
 
-        def pieces(i):
-            c0 = BANK * i
-            lead = (-c0) % DH
-            whole = (BANK - lead) // DH
-            tail = BANK - lead - whole * DH
-            runs = []
-            if lead:
-                runs.append((0, lead, c0 // DH, DH - lead))
-            runs.append((lead, whole * DH, (c0 + lead) // DH, 0))
-            if tail:
-                runs.append((BANK - tail, tail, (c0 + lead) // DH + whole, 0))
-            return runs
+            build_tables(0, 0)
+            x_now = [permute(0, t) for t in range(TOK)]
 
-        def stage_view(stage, head, n_heads):
-            j = max(k for k in range(NB) if FIRST_HEAD[k] <= head)
-            return stage[j][:, head - FIRST_HEAD[j] : head - FIRST_HEAD[j] + n_heads]
+            def pieces(i):
+                c0 = BANK * i
+                lead = (-c0) % DH
+                whole = (BANK - lead) // DH
+                tail = BANK - lead - whole * DH
+                runs = []
+                if lead:
+                    runs.append((0, lead, c0 // DH, DH - lead))
+                runs.append((lead, whole * DH, (c0 + lead) // DH, 0))
+                if tail:
+                    runs.append((BANK - tail, tail, (c0 + lead) // DH + whole, 0))
+                return runs
 
-        for c in range(NCHUNK):
-            b, cc = divmod(c, 2)
-            x_next = []
-            for part in range(3):
-                stage = [
-                    stages.tile([P, FIRST_HEAD[j + 1] - FIRST_HEAD[j], TOK, DH], F32, name="stage%d" % j, tag="stage%d" % j)
-                    for j in range(NB)
-                ]
-                dst = outs[part][b, :, CHUNK * cc : CHUNK * (cc + 1), :]
-                eng = nc.sync if part < 2 else nc.scalar
-                for i in range(NB):
-                    last = c == NCHUNK - 1 and part == 2 and i == NB - 1
-                    heads = slice(FIRST_HEAD[i], FIRST_HEAD[i + 1])
+            for c in range(NCHUNK):
+                b, cc = divmod(c, 2)
+                x_next = []
+                stage = {}
+
+                def stage_view(part, head, n_heads):
+                    j = max(k for k in range(NB) if FIRST_HEAD[k] <= head)
+                    return stage[(part, j)][:, head - FIRST_HEAD[j] : head - FIRST_HEAD[j] + n_heads]
+
+                for part, i in jobs_of(c):
+                    natural = c == 0 and part == 2
+                    by_token = natural or (c == NCHUNK - 1 and part == 2 and i == NB - 1)
+                    for j in range(i, min(i + 2, NB)):
+                        if (part, j) not in stage:
+                            stage[(part, j)] = stages.tile(
+                                [P, FIRST_HEAD[j + 1] - FIRST_HEAD[j], TOK, DH], F32, name="stage%d" % j, tag="stage%d" % j
+                            )
+                    dst = outs[part][b, FIRST_HEAD[i] : FIRST_HEAD[i + 1], CHUNK * cc : CHUNK * (cc + 1), :]
+                    eng = nc.sync if part < 2 else nc.scalar
+                    k = NB * part + i
                     if part < 2:
                         t1 = prod.tile([P, TOK, BANK], F32, name="t1", tag="t1")
                         t2 = prod.tile([P, TOK, BANK], F32, name="t2", tag="t2")
                     for t in range(TOK):
-                        xc, xs = x_now[t]
                         acc = psum.tile([P, BANK], F32, name="acc", tag="acc")
                         for g in range(G):
+                            if natural:
+                                lhsT = xr_codes[0][:, g, 2 * P * t : 2 * P * (t + 1)]
+                                lhsT_scale = xr_planes[0][:, g, P * t : P * (t + 1)]
+                            else:
+                                lhsT = x_now[t][0][:, g, :]
+                                lhsT_scale = x_now[t][1][:, g, :]
                             nc.tensor.matmul_mx(
                                 out=acc[:],
-                                lhsT=xc[:, g, :].bitcast(FP4X4),
-                                lhsT_scale=xs[:, g, :],
-                                rhs=w_codes[NB * part + i][:, g, :].bitcast(FP4X4),
-                                rhs_scale=w_planes[NB * part + i][:, g, :],
+                                lhsT=lhsT.bitcast(FP4X4),
+                                lhsT_scale=lhsT_scale,
+                                rhs=w_codes[k][:, g, :].bitcast(FP4X4),
+                                rhs_scale=w_planes[k][:, g, :],
                                 start=(g == 0),
                                 stop=(g == G - 1),
                             )
                         if part < 2:
                             tab = slice(GRP * i, GRP * i + BANK)
-                            nc.vector.tensor_tensor(
-                                out=t1[:, t, :], in0=acc[:], in1=cos_tab[(cc, t)][:, tab], op=ALU.mult
-                            )
+                            nc.vector.tensor_tensor(out=t1[:, t, :], in0=acc[:], in1=cos_tab[(cc, t)][:, tab], op=ALU.mult)
                             u = acc[:].rearrange("p (a h j) -> p a h j", h=2, j=HALF)
                             t2v = t2[:, t, :].rearrange("p (a h j) -> p a h j", h=2, j=HALF)
                             sv = sin_tab[(cc, t)][:, tab].rearrange("p (a h j) -> p a h j", h=2, j=HALF)
-                            for h in range(2):
-                                nc.vector.tensor_tensor(
-                                    out=t2v[:, :, h, :], in0=u[:, :, 1 - h, :], in1=sv[:, :, h, :], op=ALU.mult
-                                )
+                            nc.vector.tensor_tensor(out=t2v, in0=u[:, :, ::-1, :], in1=sv, op=ALU.mult)
                         else:
                             for a, n, head, d in pieces(i):
                                 if n > DH:
                                     nc.scalar.copy(
-                                        out=stage_view(stage, head, n // DH)[:, :, t, :],
+                                        out=stage_view(part, head, n // DH)[:, :, t, :],
                                         in_=acc[:, a : a + n].rearrange("p (h d) -> p h d", d=DH),
                                     )
                                 else:
-                                    nc.scalar.copy(
-                                        out=stage_view(stage, head, 1)[:, 0, t, d : d + n], in_=acc[:, a : a + n]
-                                    )
-                            if i == 0 and c + 1 < NCHUNK:
-                                x_next.append(permute(c + 1, t))
-                            if last:
+                                    nc.scalar.copy(out=stage_view(part, head, 1)[:, 0, t, d : d + n], in_=acc[:, a : a + n])
+                            if natural:
                                 eng.dma_start(
-                                    out=dst[heads].rearrange("h (p t) d -> p h t d", t=TOK)[:, :, t, :],
-                                    in_=stage[i][:, :, t, :],
+                                    out=dst[:, P * t : P * (t + 1), :].rearrange("h p d -> p h d"),
+                                    in_=stage[(part, i)][:, :, t, :],
                                 )
+                            elif by_token:
+                                eng.dma_start(
+                                    out=dst.rearrange("h (p t) d -> p h t d", t=TOK)[:, :, t, :],
+                                    in_=stage[(part, i)][:, :, t, :],
+                                )
+                            if c == 0 and i == 0 and t + 1 < TOK:
+                                build_tables(0, t + 1)
+                            if c == 0 and i == 1:
+                                build_tables(1, t)
+                            if i == 1 and c + 1 < NCHUNK:
+                                x_next.append(permute(c + 1, t))
                     if part < 2:
+                        adder = nc.vector if (c == NCHUNK - 1 and part == 1 and i == NB - 1) else nc.gpsimd
                         for a, n, head, d in pieces(i):
                             if n > DH:
-                                nc.gpsimd.tensor_tensor(
-                                    out=stage_view(stage, head, n // DH),
+                                adder.tensor_tensor(
+                                    out=stage_view(part, head, n // DH),
                                     in0=t1[:, :, a : a + n].rearrange("p t (h d) -> p h t d", d=DH),
                                     in1=t2[:, :, a : a + n].rearrange("p t (h d) -> p h t d", d=DH),
                                     op=ALU.add,
                                 )
                             else:
-                                nc.gpsimd.tensor_tensor(
-                                    out=stage_view(stage, head, 1)[:, 0, :, d : d + n],
+                                adder.tensor_tensor(
+                                    out=stage_view(part, head, 1)[:, 0, :, d : d + n],
                                     in0=t1[:, :, a : a + n],
                                     in1=t2[:, :, a : a + n],
                                     op=ALU.add,
                                 )
-                    if not last:
+                    if not by_token:
                         eng.dma_start(
-                            out=dst[heads].rearrange("h (p t) d -> p h (t d)", t=TOK),
-                            in_=stage[i][:].rearrange("p h t d -> p h (t d)"),
+                            out=dst.rearrange("h (p t) d -> p h (t d)", t=TOK),
+                            in_=stage[(part, i)][:].rearrange("p h t d -> p h (t d)"),
                         )
-            if c + 3 < NCHUNK:
-                load_x_scales(c + 3)
-                load_x_codes(c + 3)
-            x_now = x_next
+                if c + 2 < NCHUNK:
+                    load_x_scales(c + 2)
+                    load_x_codes(c + 2)
+                x_now = x_next

@@ -25,6 +25,7 @@ HALF = GRP // 2
 REP = 6
 TABW = REP * DH
 FIRST_HEAD = [0, 5, 10, 16]
+R_AT, RS_AT, L_AT, LS_AT = 0, 0, 0, 0
 
 FLOPS = 2 * 2048 * 2048 * 4608
 
@@ -40,243 +41,254 @@ def tile_attention_pa_kernel(
         xperm = ctx.enter_context(tc.tile_pool(name="xperm", bufs=2))
         prod = ctx.enter_context(tc.tile_pool(name="prod", bufs=3))
         stages = ctx.enter_context(tc.tile_pool(name="stages", bufs=2))
-        psum = ctx.enter_context(tc.psum_pool(name="psum", bufs=8))
-        with tc.manual_schedule():
+        psum = ctx.enter_context(tc.psum_pool(name="psum", bufs=1))
+        ctx.enter_context(tc.manual_schedule())
 
-            w_codes = [
-                keep.tile([P, G, 2 * BANK], U8, name="w_codes%d" % k, align_bytes=64) for k in range(3 * NB)
-            ]
-            w_planes = [keep.tile([P, G, BANK], U8, name="w_planes%d" % k, align_bytes=64) for k in range(3 * NB)]
-            xr_codes = [keep.tile([P, G, 2 * CHUNK], U8, name="xr_codes%d" % k, align_bytes=64) for k in range(2)]
-            xr_planes = [keep.tile([P, G, CHUNK], U8, name="xr_planes%d" % k, align_bytes=64) for k in range(2)]
+        def padded(pool, width, shift, name):
+            pitch = width
+            whole = pool.tile([P, shift + G * pitch], U8, name=name, tag=name, align_bytes=64)
+            return whole, whole[:, shift:].rearrange("p (g n) -> p g n", g=G)[:, :, :width]
 
-            def load_scale_rows(planes, scales):
-                for q in range(4):
-                    nc.sync.dma_start(
-                        out=planes[32 * q : 32 * q + 4, :, :].bitcast(I32),
-                        in_=scales[:, 4 * q : 4 * q + 4, :].rearrange("g r n -> r g n").bitcast(I32),
-                    )
+        w_codes = [padded(keep, 2 * BANK, R_AT, "w_codes%d" % k)[1] for k in range(3 * NB)]
+        w_plane_tiles = [padded(keep, BANK, RS_AT, "w_planes%d" % k) for k in range(3 * NB)]
+        w_planes = [view for whole, view in w_plane_tiles]
+        xr_codes = [padded(keep, 2 * CHUNK, L_AT, "xr_codes%d" % k)[1] for k in range(2)]
+        xr_plane_tiles = [padded(keep, CHUNK, LS_AT, "xr_planes%d" % k) for k in range(2)]
+        xr_planes = [view for whole, view in xr_plane_tiles]
 
-            def load_x_codes(c):
+        def load_scale_rows(planes, scales):
+            for q in range(4):
                 nc.sync.dma_start(
-                    out=xr_codes[c % 2][:].bitcast(I32),
+                    out=planes[32 * q : 32 * q + 4, :, :].bitcast(I32),
+                    in_=scales[:, 4 * q : 4 * q + 4, :].rearrange("g r n -> r g n").bitcast(I32),
+                )
+
+        def load_x(c, codes_first):
+            def codes():
+                nc.sync.dma_start(
+                    out=xr_codes[c % 2].bitcast(I32),
                     in_=x_words[:, :, 2 * CHUNK * c : 2 * CHUNK * (c + 1)].rearrange("g p n -> p g n").bitcast(I32),
                 )
 
-            def load_x_scales(c):
-                load_scale_rows(xr_planes[c % 2], x_scales[:, :, CHUNK * c : CHUNK * (c + 1)])
+            if codes_first:
+                codes()
+            load_scale_rows(xr_planes[c % 2], x_scales[:, :, CHUNK * c : CHUNK * (c + 1)])
+            if not codes_first:
+                codes()
 
-            def load_w_codes(k):
-                nc.sync.dma_start(
-                    out=w_codes[k][:].bitcast(I32),
-                    in_=Wqkv_words[:, :, 2 * BANK * k : 2 * BANK * (k + 1)].rearrange("g p n -> p g n").bitcast(I32),
-                )
-
-            def load_w_scales(k):
-                load_scale_rows(w_planes[k], Wqkv_scales[:, :, BANK * k : BANK * (k + 1)])
-
-            def permute(c, t):
-                xc = xperm.tile([P, G, 2 * P], U8, name="xc%d" % t, tag="xc%d" % t, align_bytes=64)
-                nc.vector.tensor_copy(
-                    out=xc[:].rearrange("p g (m b) -> p g m b", b=2),
-                    in_=xr_codes[c % 2][:].rearrange("p g (m t b) -> p t g m b", t=TOK, b=2)[:, t],
-                )
-                xs = xperm.tile([P, G, P], U8, name="xs%d" % t, tag="xs%d" % t, align_bytes=64)
-                nc.vector.tensor_copy(
-                    out=xs[:],
-                    in_=xr_planes[c % 2][:].rearrange("p g (m t) -> p t g m", t=TOK)[:, t],
-                )
-                return xc, xs
-
-            def jobs_of(c):
-                rope = [(part, i) for part in (0, 1) for i in range(NB)]
-                pairs = [rope[2 * j : 2 * j + 2] for j in range(NB)]
-                vals = [[(2, j)] for j in range(NB)]
-                if c == 0:
-                    groups = [vals[0], pairs[0], vals[1], pairs[1], vals[2], pairs[2]]
-                elif c == NCHUNK - 1:
-                    groups = pairs + vals
-                else:
-                    groups = [pairs[0], vals[0], pairs[1], vals[1], pairs[2], vals[2]]
-                return [job for group in groups for job in group]
-
-            warm = keep.tile([P, 1], F32, name="warm")
-            warm2 = keep.tile([P, 1], F32, name="warm2")
-            nc.gpsimd.memset(warm[:], 0.0)
-            nc.scalar.activation(out=warm2[:], in_=warm[:], func=ACT.Sin)
-
-            fraw = keep.tile([P, 3, 2, TOK, GRP], BF16, name="fraw")
-            for i, f in enumerate((f1, f2, f3)):
-                nc.gpsimd.dma_start(
-                    out=fraw[:, i].rearrange("p c t j -> p c (t j)"),
-                    in_=f.rearrange("(c p t) j -> p c (t j)", c=2, t=TOK),
-                )
-
-            first = [NB * part + i for part, i in jobs_of(0)]
-            nc.vector.memset(xr_planes[0][:].bitcast(I32), 0)
-            for k in first:
-                nc.vector.memset(w_planes[k][:].bitcast(I32), 0)
-            nc.vector.memset(xr_planes[1][:].bitcast(I32), 0)
-            load_x_codes(0)
-            load_w_codes(first[0])
-            load_x_scales(0)
-            load_w_scales(first[0])
-            for n, k in enumerate(first[1:]):
-                load_w_scales(k)
-                load_w_codes(k)
-                if n == 1:
-                    load_x_scales(1)
-                    load_x_codes(1)
-
-            half = keep.tile([P, 3, 2, TOK, GRP], F32, name="half")
-            sq = keep.tile([P, 3, 2, TOK, GRP], F32, name="sq")
-            nc.scalar.activation(
-                out=half[:].rearrange("p i c t j -> p (i c t j)"),
-                in_=fraw[:].rearrange("p i c t j -> p (i c t j)"),
-                func=ACT.Sin,
-                scale=0.5,
+        def load_w_codes(k):
+            nc.sync.dma_start(
+                out=w_codes[k].bitcast(I32),
+                in_=Wqkv_words[:, :, 2 * BANK * k : 2 * BANK * (k + 1)].rearrange("g p n -> p g n").bitcast(I32),
             )
-            nc.scalar.activation(
-                out=sq[:].rearrange("p i c t j -> p (i c t j)"),
-                in_=half[:].rearrange("p i c t j -> p (i c t j)"),
-                func=ACT.Square,
-            )
-            cos_tab = {}
-            sin_tab = {}
 
-            def build_tables(cc, t):
-                ct = keep.tile([P, TABW], F32, name="cos%d_%d" % (cc, t))
+        def load_w_scales(k):
+            load_scale_rows(w_planes[k], Wqkv_scales[:, :, BANK * k : BANK * (k + 1)])
+
+        def permute(c, t):
+            xc = padded(xperm, 2 * P, L_AT, "xc%d" % t)[1]
+            nc.vector.tensor_copy(
+                out=xc.rearrange("p g (m b) -> p g m b", b=2),
+                in_=xr_codes[c % 2].rearrange("p g (m t b) -> p t g m b", t=TOK, b=2)[:, t],
+            )
+            xs = padded(xperm, P, LS_AT, "xs%d" % t)[1]
+            nc.vector.tensor_copy(out=xs, in_=xr_planes[c % 2].rearrange("p g (m t) -> p t g m", t=TOK)[:, t])
+            return xc, xs
+
+        def jobs_of(c):
+            rope = [(part, i) for part in (0, 1) for i in range(NB)]
+            pairs = [rope[2 * j : 2 * j + 2] for j in range(NB)]
+            vals = [[(2, j)] for j in range(NB)]
+            if c == 0:
+                groups = [vals[0], pairs[0], vals[1], pairs[1], vals[2], pairs[2]]
+            elif c == NCHUNK - 1:
+                groups = pairs + vals
+            else:
+                groups = [pairs[0], vals[0], pairs[1], vals[1], pairs[2], vals[2]]
+            return [job for group in groups for job in group]
+
+        warm = keep.tile([P, 1], F32, name="warm")
+        warm2 = keep.tile([P, 1], F32, name="warm2")
+        nc.gpsimd.memset(warm[:], 0.0)
+        nc.scalar.activation(out=warm2[:], in_=warm[:], func=ACT.Sin)
+
+        fraw = keep.tile([P, 3, 2, TOK, GRP], BF16, name="fraw")
+        for i, f in enumerate((f1, f2, f3)):
+            nc.gpsimd.dma_start(
+                out=fraw[:, i].rearrange("p c t j -> p c (t j)"),
+                in_=f.rearrange("(c p t) j -> p c (t j)", c=2, t=TOK),
+            )
+
+        first = [NB * part + i for part, i in jobs_of(0)]
+        nc.vector.memset(xr_plane_tiles[0][0][:].bitcast(I32), 0)
+        for k in first:
+            nc.vector.memset(w_plane_tiles[k][0][:].bitcast(I32), 0)
+        nc.vector.memset(xr_plane_tiles[1][0][:].bitcast(I32), 0)
+        nc.sync.dma_start(
+            out=xr_codes[0].bitcast(I32),
+            in_=x_words[:, :, : 2 * CHUNK].rearrange("g p n -> p g n").bitcast(I32),
+        )
+        load_w_codes(first[0])
+        load_scale_rows(xr_planes[0], x_scales[:, :, :CHUNK])
+        load_w_scales(first[0])
+        for n, k in enumerate(first[1:]):
+            load_w_scales(k)
+            load_w_codes(k)
+            if n == 1:
+                load_x(1, False)
+
+        half = keep.tile([P, 3, 2, TOK, GRP], F32, name="half")
+        sq = keep.tile([P, 3, 2, TOK, GRP], F32, name="sq")
+        nc.scalar.activation(
+            out=half[:].rearrange("p i c t j -> p (i c t j)"),
+            in_=fraw[:].rearrange("p i c t j -> p (i c t j)"),
+            func=ACT.Sin,
+            scale=0.5,
+        )
+        nc.scalar.activation(
+            out=sq[:].rearrange("p i c t j -> p (i c t j)"),
+            in_=half[:].rearrange("p i c t j -> p (i c t j)"),
+            func=ACT.Square,
+        )
+        cos_tab = {}
+        sin_tab = {}
+
+        def build_tables(cc, t):
+            ct = keep.tile([P, TABW], F32, name="cos%d_%d" % (cc, t))
+            nc.scalar.activation(
+                out=ct[:].rearrange("p (r i j) -> p r i j", i=3, j=GRP),
+                in_=sq[:, :, cc, t, :].unsqueeze(1).to_broadcast([P, REP, 3, GRP]),
+                func=ACT.Copy,
+                scale=-2.0,
+                bias=1.0,
+            )
+            st = keep.tile([P, TABW], F32, name="sin%d_%d" % (cc, t))
+            sv = st[:].rearrange("p (r i h j) -> p r i h j", i=3, h=2, j=HALF)
+            for h, sign in ((0, -1.0), (1, 1.0)):
                 nc.scalar.activation(
-                    out=ct[:].rearrange("p (r i j) -> p r i j", i=3, j=GRP),
-                    in_=sq[:, :, cc, t, :].unsqueeze(1).to_broadcast([P, REP, 3, GRP]),
-                    func=ACT.Copy,
-                    scale=-2.0,
-                    bias=1.0,
+                    out=sv[:, :, :, h, :],
+                    in_=fraw[:, :, cc, t, HALF * h : HALF * (h + 1)].unsqueeze(1).to_broadcast([P, REP, 3, HALF]),
+                    func=ACT.Sin,
+                    scale=sign,
                 )
-                st = keep.tile([P, TABW], F32, name="sin%d_%d" % (cc, t))
-                sv = st[:].rearrange("p (r i h j) -> p r i h j", i=3, h=2, j=HALF)
-                for h, sign in ((0, -1.0), (1, 1.0)):
-                    nc.scalar.activation(
-                        out=sv[:, :, :, h, :],
-                        in_=fraw[:, :, cc, t, HALF * h : HALF * (h + 1)].unsqueeze(1).to_broadcast([P, REP, 3, HALF]),
-                        func=ACT.Sin,
-                        scale=sign,
-                    )
-                cos_tab[(cc, t)] = ct
-                sin_tab[(cc, t)] = st
+            cos_tab[(cc, t)] = ct
+            sin_tab[(cc, t)] = st
 
-            build_tables(0, 0)
-            x_now = [permute(0, t) for t in range(TOK)]
+        build_tables(0, 0)
+        x_now = [permute(0, t) for t in range(TOK)]
 
-            def pieces(i):
-                c0 = BANK * i
-                lead = (-c0) % DH
-                whole = (BANK - lead) // DH
-                tail = BANK - lead - whole * DH
-                runs = []
-                if lead:
-                    runs.append((0, lead, c0 // DH, DH - lead))
-                runs.append((lead, whole * DH, (c0 + lead) // DH, 0))
-                if tail:
-                    runs.append((BANK - tail, tail, (c0 + lead) // DH + whole, 0))
-                return runs
+        def pieces(i):
+            c0 = BANK * i
+            lead = (-c0) % DH
+            whole = (BANK - lead) // DH
+            tail = BANK - lead - whole * DH
+            runs = []
+            if lead:
+                runs.append((0, lead, c0 // DH, DH - lead))
+            runs.append((lead, whole * DH, (c0 + lead) // DH, 0))
+            if tail:
+                runs.append((BANK - tail, tail, (c0 + lead) // DH + whole, 0))
+            return runs
 
-            for c in range(NCHUNK):
-                b, cc = divmod(c, 2)
-                x_next = []
-                stage = {}
+        job = 0
+        for c in range(NCHUNK):
+            b, cc = divmod(c, 2)
+            x_next = []
+            stage = {}
 
-                def stage_view(part, head, n_heads):
-                    j = max(k for k in range(NB) if FIRST_HEAD[k] <= head)
-                    return stage[(part, j)][:, head - FIRST_HEAD[j] : head - FIRST_HEAD[j] + n_heads]
+            def stage_view(part, head, n_heads):
+                j = max(k for k in range(NB) if FIRST_HEAD[k] <= head)
+                return stage[(part, j)][:, head - FIRST_HEAD[j] : head - FIRST_HEAD[j] + n_heads]
 
-                for part, i in jobs_of(c):
-                    natural = c == 0 and part == 2
-                    by_token = natural or (c == NCHUNK - 1 and part == 2 and i == NB - 1)
-                    for j in range(i, min(i + 2, NB)):
-                        if (part, j) not in stage:
-                            stage[(part, j)] = stages.tile(
-                                [P, FIRST_HEAD[j + 1] - FIRST_HEAD[j], TOK, DH], F32, name="stage%d" % j, tag="stage%d" % j
-                            )
-                    dst = outs[part][b, FIRST_HEAD[i] : FIRST_HEAD[i + 1], CHUNK * cc : CHUNK * (cc + 1), :]
-                    eng = nc.sync if part < 2 else nc.scalar
-                    k = NB * part + i
-                    if part < 2:
-                        t1 = prod.tile([P, TOK, BANK], F32, name="t1", tag="t1")
-                        t2 = prod.tile([P, TOK, BANK], F32, name="t2", tag="t2")
-                    for t in range(TOK):
-                        acc = psum.tile([P, BANK], F32, name="acc", tag="acc")
-                        for g in range(G):
-                            if natural:
-                                lhsT = xr_codes[0][:, g, 2 * P * t : 2 * P * (t + 1)]
-                                lhsT_scale = xr_planes[0][:, g, P * t : P * (t + 1)]
-                            else:
-                                lhsT = x_now[t][0][:, g, :]
-                                lhsT_scale = x_now[t][1][:, g, :]
-                            nc.tensor.matmul_mx(
-                                out=acc[:],
-                                lhsT=lhsT.bitcast(FP4X4),
-                                lhsT_scale=lhsT_scale,
-                                rhs=w_codes[k][:, g, :].bitcast(FP4X4),
-                                rhs_scale=w_planes[k][:, g, :],
-                                start=(g == 0),
-                                stop=(g == G - 1),
-                            )
-                        if part < 2:
-                            tab = slice(GRP * i, GRP * i + BANK)
-                            nc.vector.tensor_tensor(out=t1[:, t, :], in0=acc[:], in1=cos_tab[(cc, t)][:, tab], op=ALU.mult)
-                            u = acc[:].rearrange("p (a h j) -> p a h j", h=2, j=HALF)
-                            t2v = t2[:, t, :].rearrange("p (a h j) -> p a h j", h=2, j=HALF)
-                            sv = sin_tab[(cc, t)][:, tab].rearrange("p (a h j) -> p a h j", h=2, j=HALF)
-                            nc.vector.tensor_tensor(out=t2v, in0=u[:, :, ::-1, :], in1=sv, op=ALU.mult)
+            for part, i in jobs_of(c):
+                natural = c == 0 and part == 2
+                by_token = natural or (c == NCHUNK - 1 and part == 2 and i == NB - 1)
+                for j in range(i, min(i + 2, NB)):
+                    if (part, j) not in stage:
+                        stage[(part, j)] = stages.tile(
+                            [P, FIRST_HEAD[j + 1] - FIRST_HEAD[j], TOK, DH], F32, name="stage%d" % j, tag="stage%d" % j
+                        )
+                dst = outs[part][b, FIRST_HEAD[i] : FIRST_HEAD[i + 1], CHUNK * cc : CHUNK * (cc + 1), :]
+                eng = nc.sync if part < 2 else nc.scalar
+                k = NB * part + i
+                if part < 2:
+                    t1 = prod.tile([P, TOK, BANK], F32, name="t1", tag="t1")
+                    t2 = prod.tile([P, TOK, BANK], F32, name="t2", tag="t2")
+                for t in range(TOK):
+                    bank = 2 * ((2 * job + t // 2) % 4) + (t + (2 * job + t // 2) // 4) % 2
+                    acc = psum.tile([P, BANK], F32, name="bank%d" % bank, tag="bank%d" % bank)
+                    for g in range(G):
+                        if natural:
+                            lhsT = xr_codes[0][:, g, 2 * P * t : 2 * P * (t + 1)]
+                            lhsT_scale = xr_planes[0][:, g, P * t : P * (t + 1)]
                         else:
-                            for a, n, head, d in pieces(i):
-                                if n > DH:
-                                    nc.scalar.copy(
-                                        out=stage_view(part, head, n // DH)[:, :, t, :],
-                                        in_=acc[:, a : a + n].rearrange("p (h d) -> p h d", d=DH),
-                                    )
-                                else:
-                                    nc.scalar.copy(out=stage_view(part, head, 1)[:, 0, t, d : d + n], in_=acc[:, a : a + n])
-                            if natural:
-                                eng.dma_start(
-                                    out=dst[:, P * t : P * (t + 1), :].rearrange("h p d -> p h d"),
-                                    in_=stage[(part, i)][:, :, t, :],
-                                )
-                            elif by_token:
-                                eng.dma_start(
-                                    out=dst.rearrange("h (p t) d -> p h t d", t=TOK)[:, :, t, :],
-                                    in_=stage[(part, i)][:, :, t, :],
-                                )
-                            if c == 0 and i == 0 and t + 1 < TOK:
-                                build_tables(0, t + 1)
-                            if c == 0 and i == 1:
-                                build_tables(1, t)
-                            if i == 1 and c + 1 < NCHUNK:
-                                x_next.append(permute(c + 1, t))
+                            lhsT = x_now[t][0][:, g, :]
+                            lhsT_scale = x_now[t][1][:, g, :]
+                        nc.tensor.matmul_mx(
+                            out=acc[:],
+                            lhsT=lhsT.bitcast(FP4X4),
+                            lhsT_scale=lhsT_scale,
+                            rhs=w_codes[k][:, g, :].bitcast(FP4X4),
+                            rhs_scale=w_planes[k][:, g, :],
+                            start=(g == 0),
+                            stop=(g == G - 1),
+                        )
                     if part < 2:
-                        adder = nc.vector if (c == NCHUNK - 1 and part == 1 and i == NB - 1) else nc.gpsimd
+                        tab = slice(GRP * i, GRP * i + BANK)
+                        nc.vector.tensor_tensor(out=t1[:, t, :], in0=acc[:], in1=cos_tab[(cc, t)][:, tab], op=ALU.mult)
+                        u = acc[:].rearrange("p (a h j) -> p a h j", h=2, j=HALF)
+                        t2v = t2[:, t, :].rearrange("p (a h j) -> p a h j", h=2, j=HALF)
+                        sv = sin_tab[(cc, t)][:, tab].rearrange("p (a h j) -> p a h j", h=2, j=HALF)
+                        nc.vector.tensor_tensor(out=t2v, in0=u[:, :, ::-1, :], in1=sv, op=ALU.mult)
+                    else:
                         for a, n, head, d in pieces(i):
                             if n > DH:
-                                adder.tensor_tensor(
-                                    out=stage_view(part, head, n // DH),
-                                    in0=t1[:, :, a : a + n].rearrange("p t (h d) -> p h t d", d=DH),
-                                    in1=t2[:, :, a : a + n].rearrange("p t (h d) -> p h t d", d=DH),
-                                    op=ALU.add,
+                                nc.scalar.copy(
+                                    out=stage_view(part, head, n // DH)[:, :, t, :],
+                                    in_=acc[:, a : a + n].rearrange("p (h d) -> p h d", d=DH),
                                 )
                             else:
-                                adder.tensor_tensor(
-                                    out=stage_view(part, head, 1)[:, 0, :, d : d + n],
-                                    in0=t1[:, :, a : a + n],
-                                    in1=t2[:, :, a : a + n],
-                                    op=ALU.add,
-                                )
-                    if not by_token:
-                        eng.dma_start(
-                            out=dst.rearrange("h (p t) d -> p h (t d)", t=TOK),
-                            in_=stage[(part, i)][:].rearrange("p h t d -> p h (t d)"),
-                        )
-                if c + 2 < NCHUNK:
-                    load_x_scales(c + 2)
-                    load_x_codes(c + 2)
-                x_now = x_next
+                                nc.scalar.copy(out=stage_view(part, head, 1)[:, 0, t, d : d + n], in_=acc[:, a : a + n])
+                        if natural:
+                            eng.dma_start(
+                                out=dst[:, P * t : P * (t + 1), :].rearrange("h p d -> p h d"),
+                                in_=stage[(part, i)][:, :, t, :],
+                            )
+                        elif by_token:
+                            eng.dma_start(
+                                out=dst.rearrange("h (p t) d -> p h t d", t=TOK)[:, :, t, :],
+                                in_=stage[(part, i)][:, :, t, :],
+                            )
+                        if c == 0 and i == 0 and t + 1 < TOK:
+                            build_tables(0, t + 1)
+                        if c == 0 and i == 1:
+                            build_tables(1, t)
+                if part == 2 and c + 1 < NCHUNK and i - (1 if c == 0 else 0) in (0, 1):
+                    x_next.extend([permute(c + 1, len(x_next) + n) for n in range(2)])
+                if c == 0 and part == 2 and i == NB - 1:
+                    load_x(2, False)
+                    load_x(3, False)
+                if part < 2:
+                    adder = nc.vector if (c == NCHUNK - 1 and part == 1 and i == NB - 1) else nc.gpsimd
+                    for a, n, head, d in pieces(i):
+                        if n > DH:
+                            adder.tensor_tensor(
+                                out=stage_view(part, head, n // DH),
+                                in0=t1[:, :, a : a + n].rearrange("p t (h d) -> p h t d", d=DH),
+                                in1=t2[:, :, a : a + n].rearrange("p t (h d) -> p h t d", d=DH),
+                                op=ALU.add,
+                            )
+                        else:
+                            adder.tensor_tensor(
+                                out=stage_view(part, head, 1)[:, 0, :, d : d + n],
+                                in0=t1[:, :, a : a + n],
+                                in1=t2[:, :, a : a + n],
+                                op=ALU.add,
+                            )
+                if not by_token:
+                    eng.dma_start(
+                        out=dst.rearrange("h (p t) d -> p h (t d)", t=TOK),
+                        in_=stage[(part, i)][:].rearrange("p h t d -> p h (t d)"),
+                    )
+                job += 1
+            x_now = x_next

@@ -25,7 +25,7 @@ HALF = GRP // 2
 REP = 6
 TABW = REP * DH
 FIRST_HEAD = [0, 5, 10, 16]
-R_AT, RS_AT, L_AT, LS_AT = 0, 0, 0, 0
+RAW_CODES = G * 2 * CHUNK
 
 FLOPS = 2 * 2048 * 2048 * 4608
 
@@ -38,23 +38,25 @@ def tile_attention_pa_kernel(
 
     with ExitStack() as ctx:
         keep = ctx.enter_context(tc.tile_pool(name="keep", bufs=1))
-        xperm = ctx.enter_context(tc.tile_pool(name="xperm", bufs=2))
         prod = ctx.enter_context(tc.tile_pool(name="prod", bufs=3))
         stages = ctx.enter_context(tc.tile_pool(name="stages", bufs=2))
+        vstages = ctx.enter_context(tc.tile_pool(name="vstages", bufs=1))
         psum = ctx.enter_context(tc.psum_pool(name="psum", bufs=1))
         ctx.enter_context(tc.manual_schedule())
 
-        def padded(pool, width, shift, name):
-            pitch = width
-            whole = pool.tile([P, shift + G * pitch], U8, name=name, tag=name, align_bytes=64)
-            return whole, whole[:, shift:].rearrange("p (g n) -> p g n", g=G)[:, :, :width]
+        def by_pass(flat):
+            return flat.rearrange("p (g n) -> p g n", g=G)
 
-        w_codes = [padded(keep, 2 * BANK, R_AT, "w_codes%d" % k)[1] for k in range(3 * NB)]
-        w_plane_tiles = [padded(keep, BANK, RS_AT, "w_planes%d" % k) for k in range(3 * NB)]
-        w_planes = [view for whole, view in w_plane_tiles]
-        xr_codes = [padded(keep, 2 * CHUNK, L_AT, "xr_codes%d" % k)[1] for k in range(2)]
-        xr_plane_tiles = [padded(keep, CHUNK, LS_AT, "xr_planes%d" % k) for k in range(2)]
-        xr_planes = [view for whole, view in xr_plane_tiles]
+        w_code_tiles = [keep.tile([P, G * 2 * BANK], U8, name="w_codes%d" % k, align_bytes=64) for k in range(3 * NB)]
+        w_plane_tiles = [keep.tile([P, G * BANK], U8, name="w_planes%d" % k, align_bytes=64) for k in range(3 * NB)]
+        w_codes = [by_pass(tile_[:]) for tile_ in w_code_tiles]
+        w_planes = [by_pass(tile_[:]) for tile_ in w_plane_tiles]
+        raw = [
+            prod.tile([P, RAW_CODES + G * CHUNK], U8, name="raw%d" % c, tag="t%d" % (1 + c % 2), align_bytes=64)
+            for c in range(NCHUNK)
+        ]
+        xr_codes = [by_pass(tile_[:, :RAW_CODES]) for tile_ in raw]
+        xr_planes = [by_pass(tile_[:, RAW_CODES:]) for tile_ in raw]
 
         def load_scale_rows(planes, scales):
             for q in range(4):
@@ -63,18 +65,14 @@ def tile_attention_pa_kernel(
                     in_=scales[:, 4 * q : 4 * q + 4, :].rearrange("g r n -> r g n").bitcast(I32),
                 )
 
-        def load_x(c, codes_first):
-            def codes():
-                nc.sync.dma_start(
-                    out=xr_codes[c % 2].bitcast(I32),
-                    in_=x_words[:, :, 2 * CHUNK * c : 2 * CHUNK * (c + 1)].rearrange("g p n -> p g n").bitcast(I32),
-                )
+        def load_x_codes(c):
+            nc.sync.dma_start(
+                out=xr_codes[c].bitcast(I32),
+                in_=x_words[:, :, 2 * CHUNK * c : 2 * CHUNK * (c + 1)].rearrange("g p n -> p g n").bitcast(I32),
+            )
 
-            if codes_first:
-                codes()
-            load_scale_rows(xr_planes[c % 2], x_scales[:, :, CHUNK * c : CHUNK * (c + 1)])
-            if not codes_first:
-                codes()
+        def load_x_scales(c):
+            load_scale_rows(xr_planes[c], x_scales[:, :, CHUNK * c : CHUNK * (c + 1)])
 
         def load_w_codes(k):
             nc.sync.dma_start(
@@ -85,60 +83,70 @@ def tile_attention_pa_kernel(
         def load_w_scales(k):
             load_scale_rows(w_planes[k], Wqkv_scales[:, :, BANK * k : BANK * (k + 1)])
 
-        def permute(c, t):
-            xc = padded(xperm, 2 * P, L_AT, "xc%d" % t)[1]
-            nc.vector.tensor_copy(
-                out=xc.rearrange("p g (m b) -> p g m b", b=2),
-                in_=xr_codes[c % 2].rearrange("p g (m t b) -> p t g m b", t=TOK, b=2)[:, t],
-            )
-            xs = padded(xperm, P, LS_AT, "xs%d" % t)[1]
-            nc.vector.tensor_copy(out=xs, in_=xr_planes[c % 2].rearrange("p g (m t) -> p t g m", t=TOK)[:, t])
-            return xc, xs
+        def zero_x_planes(c):
+            nc.vector.memset(raw[c][:, RAW_CODES:].bitcast(I32), 0)
 
-        def jobs_of(c):
-            rope = [(part, i) for part in (0, 1) for i in range(NB)]
-            pairs = [rope[2 * j : 2 * j + 2] for j in range(NB)]
-            vals = [[(2, j)] for j in range(NB)]
-            if c == 0:
-                groups = [vals[0], pairs[0], vals[1], pairs[1], vals[2], pairs[2]]
-            elif c == NCHUNK - 1:
-                groups = pairs + vals
-            else:
-                groups = [pairs[0], vals[0], pairs[1], vals[1], pairs[2], vals[2]]
-            return [job for group in groups for job in group]
+        def zero_w_planes(k):
+            nc.vector.memset(w_plane_tiles[k][:].bitcast(I32), 0)
+
+        def permute(c, t):
+            xc = keep.tile([P, G * 2 * P], U8, name="xc%d_%d" % (c, t), align_bytes=64)
+            nc.vector.tensor_copy(
+                out=by_pass(xc[:]).rearrange("p g (m b) -> p g m b", b=2),
+                in_=xr_codes[c].rearrange("p g (m t b) -> p t g m b", t=TOK, b=2)[:, t],
+            )
+            xs = keep.tile([P, G * P], U8, name="xs%d_%d" % (c, t), align_bytes=64)
+            nc.vector.tensor_copy(out=by_pass(xs[:]), in_=xr_planes[c].rearrange("p g (m t) -> p t g m", t=TOK)[:, t])
+            return by_pass(xc[:]), by_pass(xs[:])
+
+        rope_jobs = [(c, part, i) for c in range(NCHUNK) for part in (0, 1) for i in range(NB)]
+        value_jobs = [(c, 2, i) for c in range(NCHUNK) for i in range(NB)]
+        woven = value_jobs[NB:-NB]
+        order = value_jobs[:NB]
+        placed = 0
+        for r, rope_job in enumerate(rope_jobs):
+            order.append(rope_job)
+            if placed < len(woven) and (r + 1) * (len(woven) + 1) >= (placed + 1) * len(rope_jobs):
+                order.append(woven[placed])
+                placed += 1
+        order.extend(value_jobs[-NB:])
 
         warm = keep.tile([P, 1], F32, name="warm")
         warm2 = keep.tile([P, 1], F32, name="warm2")
         nc.gpsimd.memset(warm[:], 0.0)
-        nc.scalar.activation(out=warm2[:], in_=warm[:], func=ACT.Sin)
-
         fraw = keep.tile([P, 3, 2, TOK, GRP], BF16, name="fraw")
         for i, f in enumerate((f1, f2, f3)):
-            nc.gpsimd.dma_start(
+            nc.scalar.dma_start(
                 out=fraw[:, i].rearrange("p c t j -> p c (t j)"),
                 in_=f.rearrange("(c p t) j -> p c (t j)", c=2, t=TOK),
             )
+        nc.scalar.activation(out=warm2[:], in_=warm[:], func=ACT.Sin)
 
-        first = [NB * part + i for part, i in jobs_of(0)]
-        nc.vector.memset(xr_plane_tiles[0][0][:].bitcast(I32), 0)
-        for k in first:
-            nc.vector.memset(w_plane_tiles[k][0][:].bitcast(I32), 0)
-        nc.vector.memset(xr_plane_tiles[1][0][:].bitcast(I32), 0)
-        nc.sync.dma_start(
-            out=xr_codes[0].bitcast(I32),
-            in_=x_words[:, :, : 2 * CHUNK].rearrange("g p n -> p g n").bitcast(I32),
-        )
-        load_w_codes(first[0])
-        load_scale_rows(xr_planes[0], x_scales[:, :, :CHUNK])
-        load_w_scales(first[0])
-        for n, k in enumerate(first[1:]):
-            load_w_scales(k)
-            load_w_codes(k)
-            if n == 1:
-                load_x(1, False)
+        strips = []
+        for c, part, i in order:
+            if NB * part + i not in strips:
+                strips.append(NB * part + i)
+        loads = [("x", 0), ("w", strips[0]), ("w", strips[1]), ("x", 1), ("x", 2), ("w", strips[2]), ("x", 3)]
+        loads.extend([("w", k) for k in strips[3:]])
+        for kind, n in loads:
+            if kind == "x":
+                zero_x_planes(n)
+            else:
+                zero_w_planes(n)
+        load_x_codes(0)
+        load_w_codes(strips[0])
+        load_x_scales(0)
+        load_w_scales(strips[0])
+        for kind, n in loads[2:]:
+            if kind == "x":
+                load_x_scales(n)
+                load_x_codes(n)
+            else:
+                load_w_scales(n)
+                load_w_codes(n)
 
-        half = keep.tile([P, 3, 2, TOK, GRP], F32, name="half")
-        sq = keep.tile([P, 3, 2, TOK, GRP], F32, name="sq")
+        half = stages.tile([P, 3, 2, TOK, GRP], F32, name="half", tag="stage0")
+        sq = stages.tile([P, 3, 2, TOK, GRP], F32, name="sq", tag="stage1")
         nc.scalar.activation(
             out=half[:].rearrange("p i c t j -> p (i c t j)"),
             in_=fraw[:].rearrange("p i c t j -> p (i c t j)"),
@@ -174,8 +182,10 @@ def tile_attention_pa_kernel(
             cos_tab[(cc, t)] = ct
             sin_tab[(cc, t)] = st
 
-        build_tables(0, 0)
-        x_now = [permute(0, t) for t in range(TOK)]
+        for t in range(TOK):
+            build_tables(0, t)
+
+        x_tiles = [[permute(c, t) for t in range(TOK)] for c in range(NCHUNK)]
 
         def pieces(i):
             c0 = BANK * i
@@ -190,105 +200,95 @@ def tile_attention_pa_kernel(
                 runs.append((BANK - tail, tail, (c0 + lead) // DH + whole, 0))
             return runs
 
-        job = 0
-        for c in range(NCHUNK):
+        stage = {}
+
+        def stage_view(c, part, head, n_heads):
+            j = max(k for k in range(NB) if FIRST_HEAD[k] <= head)
+            return stage[(c, part, j)][:, head - FIRST_HEAD[j] : head - FIRST_HEAD[j] + n_heads]
+
+        for job, (c, part, i) in enumerate(order):
             b, cc = divmod(c, 2)
-            x_next = []
-            stage = {}
-
-            def stage_view(part, head, n_heads):
-                j = max(k for k in range(NB) if FIRST_HEAD[k] <= head)
-                return stage[(part, j)][:, head - FIRST_HEAD[j] : head - FIRST_HEAD[j] + n_heads]
-
-            for part, i in jobs_of(c):
-                natural = c == 0 and part == 2
-                by_token = natural or (c == NCHUNK - 1 and part == 2 and i == NB - 1)
-                for j in range(i, min(i + 2, NB)):
-                    if (part, j) not in stage:
-                        stage[(part, j)] = stages.tile(
-                            [P, FIRST_HEAD[j + 1] - FIRST_HEAD[j], TOK, DH], F32, name="stage%d" % j, tag="stage%d" % j
-                        )
-                dst = outs[part][b, FIRST_HEAD[i] : FIRST_HEAD[i + 1], CHUNK * cc : CHUNK * (cc + 1), :]
-                eng = nc.sync if part < 2 else nc.scalar
-                k = NB * part + i
-                if part < 2:
-                    t1 = prod.tile([P, TOK, BANK], F32, name="t1", tag="t1")
-                    t2 = prod.tile([P, TOK, BANK], F32, name="t2", tag="t2")
-                for t in range(TOK):
-                    bank = 2 * ((2 * job + t // 2) % 4) + (t + (2 * job + t // 2) // 4) % 2
-                    acc = psum.tile([P, BANK], F32, name="bank%d" % bank, tag="bank%d" % bank)
-                    for g in range(G):
-                        if natural:
-                            lhsT = xr_codes[0][:, g, 2 * P * t : 2 * P * (t + 1)]
-                            lhsT_scale = xr_planes[0][:, g, P * t : P * (t + 1)]
-                        else:
-                            lhsT = x_now[t][0][:, g, :]
-                            lhsT_scale = x_now[t][1][:, g, :]
-                        nc.tensor.matmul_mx(
-                            out=acc[:],
-                            lhsT=lhsT.bitcast(FP4X4),
-                            lhsT_scale=lhsT_scale,
-                            rhs=w_codes[k][:, g, :].bitcast(FP4X4),
-                            rhs_scale=w_planes[k][:, g, :],
-                            start=(g == 0),
-                            stop=(g == G - 1),
-                        )
-                    if part < 2:
-                        tab = slice(GRP * i, GRP * i + BANK)
-                        nc.vector.tensor_tensor(out=t1[:, t, :], in0=acc[:], in1=cos_tab[(cc, t)][:, tab], op=ALU.mult)
-                        u = acc[:].rearrange("p (a h j) -> p a h j", h=2, j=HALF)
-                        t2v = t2[:, t, :].rearrange("p (a h j) -> p a h j", h=2, j=HALF)
-                        sv = sin_tab[(cc, t)][:, tab].rearrange("p (a h j) -> p a h j", h=2, j=HALF)
-                        nc.vector.tensor_tensor(out=t2v, in0=u[:, :, ::-1, :], in1=sv, op=ALU.mult)
+            natural = c == 0 and part == 2
+            by_token = natural or job == len(order) - 1
+            pool, prefix = (vstages, "vstage") if part == 2 else (stages, "stage")
+            for j in range(i, min(i + 2, NB)):
+                if (c, part, j) not in stage:
+                    stage[(c, part, j)] = pool.tile(
+                        [P, FIRST_HEAD[j + 1] - FIRST_HEAD[j], TOK, DH], F32, name="%s%d" % (prefix, j), tag="%s%d" % (prefix, j)
+                    )
+            dst = outs[part][b, FIRST_HEAD[i] : FIRST_HEAD[i + 1], CHUNK * cc : CHUNK * (cc + 1), :]
+            eng = nc.sync if part < 2 else nc.scalar
+            k = NB * part + i
+            if part < 2:
+                t1 = prod.tile([P, TOK, BANK], F32, name="t1", tag="t1", align_bytes=64)
+                t2 = prod.tile([P, TOK, BANK], F32, name="t2", tag="t2", align_bytes=64)
+            for t in range(TOK):
+                bank = 2 * ((2 * job + t // 2) % 4) + (t + (2 * job + t // 2) // 4) % 2
+                acc = psum.tile([P, BANK], F32, name="bank%d" % bank, tag="bank%d" % bank)
+                for g in range(G):
+                    if natural:
+                        lhsT = xr_codes[0][:, g, 2 * P * t : 2 * P * (t + 1)]
+                        lhsT_scale = xr_planes[0][:, g, P * t : P * (t + 1)]
                     else:
-                        for a, n, head, d in pieces(i):
-                            if n > DH:
-                                nc.scalar.copy(
-                                    out=stage_view(part, head, n // DH)[:, :, t, :],
-                                    in_=acc[:, a : a + n].rearrange("p (h d) -> p h d", d=DH),
-                                )
-                            else:
-                                nc.scalar.copy(out=stage_view(part, head, 1)[:, 0, t, d : d + n], in_=acc[:, a : a + n])
-                        if natural:
-                            eng.dma_start(
-                                out=dst[:, P * t : P * (t + 1), :].rearrange("h p d -> p h d"),
-                                in_=stage[(part, i)][:, :, t, :],
-                            )
-                        elif by_token:
-                            eng.dma_start(
-                                out=dst.rearrange("h (p t) d -> p h t d", t=TOK)[:, :, t, :],
-                                in_=stage[(part, i)][:, :, t, :],
-                            )
-                        if c == 0 and i == 0 and t + 1 < TOK:
-                            build_tables(0, t + 1)
-                        if c == 0 and i == 1:
-                            build_tables(1, t)
-                if part == 2 and c + 1 < NCHUNK and i - (1 if c == 0 else 0) in (0, 1):
-                    x_next.extend([permute(c + 1, len(x_next) + n) for n in range(2)])
-                if c == 0 and part == 2 and i == NB - 1:
-                    load_x(2, False)
-                    load_x(3, False)
+                        lhsT = x_tiles[c][t][0][:, g, :]
+                        lhsT_scale = x_tiles[c][t][1][:, g, :]
+                    nc.tensor.matmul_mx(
+                        out=acc[:],
+                        lhsT=lhsT.bitcast(FP4X4),
+                        lhsT_scale=lhsT_scale,
+                        rhs=w_codes[k][:, g, :].bitcast(FP4X4),
+                        rhs_scale=w_planes[k][:, g, :],
+                        start=(g == 0),
+                        stop=(g == G - 1),
+                    )
                 if part < 2:
-                    adder = nc.vector if (c == NCHUNK - 1 and part == 1 and i == NB - 1) else nc.gpsimd
+                    tab = slice(GRP * i, GRP * i + BANK)
+                    nc.vector.tensor_tensor(out=t1[:, t, :], in0=acc[:], in1=cos_tab[(cc, t)][:, tab], op=ALU.mult)
+                    u = acc[:].rearrange("p (a h j) -> p a h j", h=2, j=HALF)
+                    t2v = t2[:, t, :].rearrange("p (a h j) -> p a h j", h=2, j=HALF)
+                    sv = sin_tab[(cc, t)][:, tab].rearrange("p (a h j) -> p a h j", h=2, j=HALF)
+                    nc.vector.tensor_tensor(out=t2v, in0=u[:, :, ::-1, :], in1=sv, op=ALU.mult)
+                else:
                     for a, n, head, d in pieces(i):
                         if n > DH:
-                            adder.tensor_tensor(
-                                out=stage_view(part, head, n // DH),
-                                in0=t1[:, :, a : a + n].rearrange("p t (h d) -> p h t d", d=DH),
-                                in1=t2[:, :, a : a + n].rearrange("p t (h d) -> p h t d", d=DH),
-                                op=ALU.add,
+                            nc.scalar.copy(
+                                out=stage_view(c, part, head, n // DH)[:, :, t, :],
+                                in_=acc[:, a : a + n].rearrange("p (h d) -> p h d", d=DH),
                             )
                         else:
-                            adder.tensor_tensor(
-                                out=stage_view(part, head, 1)[:, 0, :, d : d + n],
-                                in0=t1[:, :, a : a + n],
-                                in1=t2[:, :, a : a + n],
-                                op=ALU.add,
-                            )
-                if not by_token:
-                    eng.dma_start(
-                        out=dst.rearrange("h (p t) d -> p h (t d)", t=TOK),
-                        in_=stage[(part, i)][:].rearrange("p h t d -> p h (t d)"),
-                    )
-                job += 1
-            x_now = x_next
+                            nc.scalar.copy(out=stage_view(c, part, head, 1)[:, 0, t, d : d + n], in_=acc[:, a : a + n])
+                    if natural:
+                        nc.sync.dma_start(
+                            out=dst[:, P * t : P * (t + 1), :].rearrange("h p d -> p h d"),
+                            in_=stage[(c, part, i)][:, :, t, :],
+                        )
+                    elif by_token:
+                        eng.dma_start(
+                            out=dst.rearrange("h (p t) d -> p h t d", t=TOK)[:, :, t, :],
+                            in_=stage[(c, part, i)][:, :, t, :],
+                        )
+            if job == NB - 1:
+                for t in range(TOK):
+                    build_tables(1, t)
+            if part < 2:
+                adder = nc.vector if (c, part, i) == rope_jobs[-1] else nc.gpsimd
+                for a, n, head, d in pieces(i):
+                    if n > DH:
+                        adder.tensor_tensor(
+                            out=stage_view(c, part, head, n // DH),
+                            in0=t1[:, :, a : a + n].rearrange("p t (h d) -> p h t d", d=DH),
+                            in1=t2[:, :, a : a + n].rearrange("p t (h d) -> p h t d", d=DH),
+                            op=ALU.add,
+                        )
+                    else:
+                        adder.tensor_tensor(
+                            out=stage_view(c, part, head, 1)[:, 0, :, d : d + n],
+                            in0=t1[:, :, a : a + n],
+                            in1=t2[:, :, a : a + n],
+                            op=ALU.add,
+                        )
+            if not by_token:
+                eng.dma_start(
+                    out=dst.rearrange("h (p t) d -> p h (t d)", t=TOK),
+                    in_=stage[(c, part, i)][:].rearrange("p h t d -> p h (t d)"),
+                )

@@ -26,6 +26,8 @@ REP = 6
 TABW = REP * DH
 FIRST_HEAD = [0, 5, 10, 16]
 RAW_CODES = G * 2 * CHUNK
+SPINS = 12
+LAST_N = 128
 
 FLOPS = 2 * 2048 * 2048 * 4608
 
@@ -114,6 +116,11 @@ def tile_attention_pa_kernel(
         warm = keep.tile([P, 1], F32, name="warm")
         warm2 = keep.tile([P, 1], F32, name="warm2")
         nc.gpsimd.memset(warm[:], 0.0)
+        idle = keep.tile([P, BANK], BF16, name="idle")
+        nc.gpsimd.memset(idle[:], 0.0)
+        spin = psum.tile([P, BANK], F32, name="bank7", tag="bank7")
+        for n in range(SPINS):
+            nc.tensor.matmul(out=spin[:], lhsT=idle[:, :P], rhs=idle[:], start=True, stop=True)
         fraw = keep.tile([P, 3, 2, TOK, GRP], BF16, name="fraw")
         for i, f in enumerate((f1, f2, f3)):
             nc.scalar.dma_start(
@@ -133,10 +140,22 @@ def tile_attention_pa_kernel(
                 zero_x_planes(n)
             else:
                 zero_w_planes(n)
-        load_x_codes(0)
-        load_w_codes(strips[0])
+        first_k = strips[0]
+        x_first = keep.tile([P, G * 2 * P], U8, name="x_first", align_bytes=64)
+        nc.sync.dma_start(
+            out=w_codes[first_k][:, : G // 2, :].bitcast(I32),
+            in_=Wqkv_words[: G // 2, :, 2 * BANK * first_k : 2 * BANK * (first_k + 1)].rearrange("g p n -> p g n").bitcast(I32),
+        )
+        nc.sync.dma_start(
+            out=by_pass(x_first[:]).bitcast(I32), in_=x_words[:, :, : 2 * P].rearrange("g p n -> p g n").bitcast(I32)
+        )
         load_x_scales(0)
-        load_w_scales(strips[0])
+        load_w_scales(first_k)
+        nc.sync.dma_start(
+            out=w_codes[first_k][:, G // 2 :, :].bitcast(I32),
+            in_=Wqkv_words[G // 2 :, :, 2 * BANK * first_k : 2 * BANK * (first_k + 1)].rearrange("g p n -> p g n").bitcast(I32),
+        )
+        load_x_codes(0)
         for kind, n in loads[2:]:
             if kind == "x":
                 load_x_scales(n)
@@ -187,18 +206,22 @@ def tile_attention_pa_kernel(
 
         x_tiles = [[permute(c, t) for t in range(TOK)] for c in range(NCHUNK)]
 
-        def pieces(i):
-            c0 = BANK * i
-            lead = (-c0) % DH
-            whole = (BANK - lead) // DH
-            tail = BANK - lead - whole * DH
+        def pieces(c0, width):
+            lead = min((-c0) % DH, width)
+            whole = (width - lead) // DH
+            tail = width - lead - whole * DH
             runs = []
             if lead:
-                runs.append((0, lead, c0 // DH, DH - lead))
-            runs.append((lead, whole * DH, (c0 + lead) // DH, 0))
+                runs.append((0, lead, c0 // DH, c0 % DH))
+            if whole:
+                runs.append((lead, whole * DH, (c0 + lead) // DH, 0))
             if tail:
-                runs.append((BANK - tail, tail, (c0 + lead) // DH + whole, 0))
+                runs.append((width - tail, tail, (c0 + lead) // DH + whole, 0))
             return runs
+
+        def bank_of(job, t):
+            pair = 2 * job + t // 2
+            return 2 * (pair % 4) + (t + pair // 4) % 2
 
         stage = {}
 
@@ -223,56 +246,69 @@ def tile_attention_pa_kernel(
                 t1 = prod.tile([P, TOK, BANK], F32, name="t1", tag="t1", align_bytes=64)
                 t2 = prod.tile([P, TOK, BANK], F32, name="t2", tag="t2", align_bytes=64)
             for t in range(TOK):
-                bank = 2 * ((2 * job + t // 2) % 4) + (t + (2 * job + t // 2) // 4) % 2
-                acc = psum.tile([P, BANK], F32, name="bank%d" % bank, tag="bank%d" % bank)
-                for g in range(G):
-                    if natural:
-                        lhsT = xr_codes[0][:, g, 2 * P * t : 2 * P * (t + 1)]
-                        lhsT_scale = xr_planes[0][:, g, P * t : P * (t + 1)]
-                    else:
-                        lhsT = x_tiles[c][t][0][:, g, :]
-                        lhsT_scale = x_tiles[c][t][1][:, g, :]
-                    nc.tensor.matmul_mx(
-                        out=acc[:],
-                        lhsT=lhsT.bitcast(FP4X4),
-                        lhsT_scale=lhsT_scale,
-                        rhs=w_codes[k][:, g, :].bitcast(FP4X4),
-                        rhs_scale=w_planes[k][:, g, :],
-                        start=(g == 0),
-                        stop=(g == G - 1),
-                    )
-                if part < 2:
-                    tab = slice(GRP * i, GRP * i + BANK)
-                    nc.vector.tensor_tensor(out=t1[:, t, :], in0=acc[:], in1=cos_tab[(cc, t)][:, tab], op=ALU.mult)
-                    u = acc[:].rearrange("p (a h j) -> p a h j", h=2, j=HALF)
-                    t2v = t2[:, t, :].rearrange("p (a h j) -> p a h j", h=2, j=HALF)
-                    sv = sin_tab[(cc, t)][:, tab].rearrange("p (a h j) -> p a h j", h=2, j=HALF)
-                    nc.vector.tensor_tensor(out=t2v, in0=u[:, :, ::-1, :], in1=sv, op=ALU.mult)
+                if job == len(order) - 1 and t == TOK - 1:
+                    windows = [
+                        (LAST_N * n, LAST_N, bank_of(job, t) if n == 0 else bank_of(job - 1, n - 1))
+                        for n in range(BANK // LAST_N)
+                    ]
                 else:
-                    for a, n, head, d in pieces(i):
+                    windows = [(0, BANK, bank_of(job, t))]
+                for w, (a0, width, bank) in enumerate(windows):
+                    acc = psum.tile([P, width], F32, name="bank%d" % bank, tag="bank%d" % bank)
+                    for g in range(G):
+                        if job == 0 and t == 0:
+                            lhsT = by_pass(x_first[:])[:, g, :]
+                            lhsT_scale = xr_planes[0][:, g, :P]
+                        elif natural:
+                            lhsT = xr_codes[0][:, g, 2 * P * t : 2 * P * (t + 1)]
+                            lhsT_scale = xr_planes[0][:, g, P * t : P * (t + 1)]
+                        else:
+                            lhsT = x_tiles[c][t][0][:, g, :]
+                            lhsT_scale = x_tiles[c][t][1][:, g, :]
+                        nc.tensor.matmul_mx(
+                            out=acc[:],
+                            lhsT=lhsT.bitcast(FP4X4),
+                            lhsT_scale=lhsT_scale,
+                            rhs=w_codes[k][:, g, 2 * a0 : 2 * (a0 + width)].bitcast(FP4X4),
+                            rhs_scale=w_planes[k][:, g, a0 : a0 + width],
+                            start=(g == 0),
+                            stop=(g == G - 1),
+                        )
+                    if part < 2:
+                        tab = slice(GRP * i, GRP * i + BANK)
+                        nc.vector.tensor_tensor(out=t1[:, t, :], in0=acc[:], in1=cos_tab[(cc, t)][:, tab], op=ALU.mult)
+                        u = acc[:].rearrange("p (a h j) -> p a h j", h=2, j=HALF)
+                        t2v = t2[:, t, :].rearrange("p (a h j) -> p a h j", h=2, j=HALF)
+                        sv = sin_tab[(cc, t)][:, tab].rearrange("p (a h j) -> p a h j", h=2, j=HALF)
+                        nc.vector.tensor_tensor(out=t2v, in0=u[:, :, ::-1, :], in1=sv, op=ALU.mult)
+                        continue
+                    by_vector = len(windows) > 1 and w % 2 == 0
+                    copy_out = nc.vector.tensor_copy if by_vector else nc.scalar.copy
+                    for a, n, head, d in pieces(BANK * i + a0, width):
                         if n > DH:
-                            nc.scalar.copy(
+                            copy_out(
                                 out=stage_view(c, part, head, n // DH)[:, :, t, :],
                                 in_=acc[:, a : a + n].rearrange("p (h d) -> p h d", d=DH),
                             )
                         else:
-                            nc.scalar.copy(out=stage_view(c, part, head, 1)[:, 0, t, d : d + n], in_=acc[:, a : a + n])
+                            copy_out(out=stage_view(c, part, head, 1)[:, 0, t, d : d + n], in_=acc[:, a : a + n])
+                    h0, h1 = (BANK * i + a0) // DH - FIRST_HEAD[i], (BANK * i + a0 + width) // DH - FIRST_HEAD[i]
                     if natural:
                         nc.sync.dma_start(
                             out=dst[:, P * t : P * (t + 1), :].rearrange("h p d -> p h d"),
                             in_=stage[(c, part, i)][:, :, t, :],
                         )
                     elif by_token:
-                        eng.dma_start(
-                            out=dst.rearrange("h (p t) d -> p h t d", t=TOK)[:, :, t, :],
-                            in_=stage[(c, part, i)][:, :, t, :],
+                        (nc.sync if by_vector else nc.scalar).dma_start(
+                            out=dst[h0:h1].rearrange("h (p t) d -> p h t d", t=TOK)[:, :, t, :],
+                            in_=stage[(c, part, i)][:, h0:h1, t, :],
                         )
             if job == NB - 1:
                 for t in range(TOK):
                     build_tables(1, t)
             if part < 2:
                 adder = nc.vector if (c, part, i) == rope_jobs[-1] else nc.gpsimd
-                for a, n, head, d in pieces(i):
+                for a, n, head, d in pieces(BANK * i, BANK):
                     if n > DH:
                         adder.tensor_tensor(
                             out=stage_view(c, part, head, n // DH),

@@ -28,6 +28,7 @@ FIRST_HEAD = [0, 5, 10, 16]
 RAW_CODES = G * 2 * CHUNK
 SPINS = 12
 LAST_N = 128
+HEAD_JOBS = 2 * NB
 
 FLOPS = 2 * 2048 * 2048 * 4608
 
@@ -103,8 +104,8 @@ def tile_attention_pa_kernel(
 
         rope_jobs = [(c, part, i) for c in range(NCHUNK) for part in (0, 1) for i in range(NB)]
         value_jobs = [(c, 2, i) for c in range(NCHUNK) for i in range(NB)]
-        woven = value_jobs[NB:-NB]
-        order = value_jobs[:NB]
+        woven = value_jobs[HEAD_JOBS:-NB]
+        order = value_jobs[:HEAD_JOBS]
         placed = 0
         for r, rope_job in enumerate(rope_jobs):
             order.append(rope_job)
@@ -133,8 +134,7 @@ def tile_attention_pa_kernel(
         for c, part, i in order:
             if NB * part + i not in strips:
                 strips.append(NB * part + i)
-        loads = [("x", 0), ("w", strips[0]), ("w", strips[1]), ("x", 1), ("x", 2), ("w", strips[2]), ("x", 3)]
-        loads.extend([("w", k) for k in strips[3:]])
+        loads = [("x", 0), ("w", strips[0]), ("w", strips[1]), ("x", 1), ("w", strips[2]), ("x", 2), ("x", 3)]
         for kind, n in loads:
             if kind == "x":
                 zero_x_planes(n)
@@ -204,7 +204,15 @@ def tile_attention_pa_kernel(
         for t in range(TOK):
             build_tables(0, t)
 
-        x_tiles = [[permute(c, t) for t in range(TOK)] for c in range(NCHUNK)]
+        x_tiles = {}
+        x_tiles[1] = [permute(1, t) for t in range(TOK)]
+        for k in strips[3:]:
+            zero_w_planes(k)
+        for k in strips[3:]:
+            load_w_scales(k)
+            load_w_codes(k)
+        for c in (0, 2, 3):
+            x_tiles[c] = [permute(c, t) for t in range(TOK)]
 
         def pieces(c0, width):
             lead = min((-c0) % DH, width)
@@ -233,7 +241,7 @@ def tile_attention_pa_kernel(
             b, cc = divmod(c, 2)
             natural = c == 0 and part == 2
             by_token = natural or job == len(order) - 1
-            pool, prefix = (vstages, "vstage") if part == 2 else (stages, "stage")
+            pool, prefix = (vstages, "vstage") if part == 2 and not natural else (stages, "stage")
             for j in range(i, min(i + 2, NB)):
                 if (c, part, j) not in stage:
                     stage[(c, part, j)] = pool.tile(
@@ -303,7 +311,7 @@ def tile_attention_pa_kernel(
                             out=dst[h0:h1].rearrange("h (p t) d -> p h t d", t=TOK)[:, :, t, :],
                             in_=stage[(c, part, i)][:, h0:h1, t, :],
                         )
-            if job == NB - 1:
+            if job == HEAD_JOBS - 1:
                 for t in range(TOK):
                     build_tables(1, t)
             if part < 2:

@@ -28,7 +28,8 @@ FIRST_HEAD = [0, 5, 10, 16]
 RAW_CODES = G * 2 * CHUNK
 SPINS = 12
 LAST_N = 128
-HEAD_JOBS = 2 * NB
+HEAD_JOBS = 4
+TAIL_JOBS = 5
 
 FLOPS = 2 * 2048 * 2048 * 4608
 
@@ -104,7 +105,7 @@ def tile_attention_pa_kernel(
 
         rope_jobs = [(c, part, i) for c in range(NCHUNK) for part in (0, 1) for i in range(NB)]
         value_jobs = [(c, 2, i) for c in range(NCHUNK) for i in range(NB)]
-        woven = value_jobs[HEAD_JOBS:-NB]
+        woven = value_jobs[HEAD_JOBS:-TAIL_JOBS]
         order = value_jobs[:HEAD_JOBS]
         placed = 0
         for r, rope_job in enumerate(rope_jobs):
@@ -112,7 +113,7 @@ def tile_attention_pa_kernel(
             if placed < len(woven) and (r + 1) * (len(woven) + 1) >= (placed + 1) * len(rope_jobs):
                 order.append(woven[placed])
                 placed += 1
-        order.extend(value_jobs[-NB:])
+        order.extend(value_jobs[-TAIL_JOBS:])
 
         warm = keep.tile([P, 1], F32, name="warm")
         warm2 = keep.tile([P, 1], F32, name="warm2")

@@ -27,7 +27,7 @@ TABW = REP * DH
 FIRST_HEAD = [0, 5, 10, 16]
 RAW_CODES = G * 2 * CHUNK
 SPINS = 12
-LAST_N = 128
+LAST_N = 512
 HEAD_JOBS = 4
 TAIL_JOBS = 5
 

@@ -307,10 +307,10 @@ def tile_attention_pa_kernel(
                             out=dst[:, P * t : P * (t + 1), :].rearrange("h p d -> p h d"),
                             in_=stage[(c, part, i)][:, :, t, :],
                         )
-                    elif by_token:
-                        (nc.sync if by_vector else nc.scalar).dma_start(
-                            out=dst[h0:h1].rearrange("h (p t) d -> p h t d", t=TOK)[:, :, t, :],
-                            in_=stage[(c, part, i)][:, h0:h1, t, :],
+                    elif by_token and t % 2 == 1:
+                        nc.scalar.dma_start(
+                            out=dst.rearrange("h (p t) d -> p h t d", t=TOK)[:, :, t - 1 : t + 1, :].rearrange("p h t d -> p h (t d)"),
+                            in_=stage[(c, part, i)][:, :, t - 1 : t + 1, :].rearrange("p h t d -> p h (t d)"),
                         )
             if job == HEAD_JOBS - 1:
                 for t in range(TOK):

@@ -26,7 +26,7 @@ REP = 6
 TABW = REP * DH
 FIRST_HEAD = [0, 5, 10, 16]
 RAW_CODES = G * 2 * CHUNK
-SPINS = 12
+SPINS = 8
 LAST_N = 512
 HEAD_JOBS = 4
 TAIL_JOBS = 5
@@ -62,12 +62,15 @@ def tile_attention_pa_kernel(
         xr_codes = [by_pass(tile_[:, :RAW_CODES]) for tile_ in raw]
         xr_planes = [by_pass(tile_[:, RAW_CODES:]) for tile_ in raw]
 
+        def load_scale_quadrant(planes, scales, q):
+            nc.sync.dma_start(
+                out=planes[32 * q : 32 * q + 4, :, :].bitcast(I32),
+                in_=scales[:, 4 * q : 4 * q + 4, :].rearrange("g r n -> r g n").bitcast(I32),
+            )
+
         def load_scale_rows(planes, scales):
             for q in range(4):
-                nc.sync.dma_start(
-                    out=planes[32 * q : 32 * q + 4, :, :].bitcast(I32),
-                    in_=scales[:, 4 * q : 4 * q + 4, :].rearrange("g r n -> r g n").bitcast(I32),
-                )
+                load_scale_quadrant(planes, scales, q)
 
         def load_x_codes(c):
             nc.sync.dma_start(
@@ -142,21 +145,30 @@ def tile_attention_pa_kernel(
             else:
                 zero_w_planes(n)
         first_k = strips[0]
-        x_first = keep.tile([P, G * 2 * P], U8, name="x_first", align_bytes=64)
-        nc.sync.dma_start(
-            out=w_codes[first_k][:, : G // 2, :].bitcast(I32),
-            in_=Wqkv_words[: G // 2, :, 2 * BANK * first_k : 2 * BANK * (first_k + 1)].rearrange("g p n -> p g n").bitcast(I32),
-        )
-        nc.sync.dma_start(
-            out=by_pass(x_first[:]).bitcast(I32), in_=x_words[:, :, : 2 * P].rearrange("g p n -> p g n").bitcast(I32)
-        )
-        load_x_scales(0)
-        load_w_scales(first_k)
-        nc.sync.dma_start(
-            out=w_codes[first_k][:, G // 2 :, :].bitcast(I32),
-            in_=Wqkv_words[G // 2 :, :, 2 * BANK * first_k : 2 * BANK * (first_k + 1)].rearrange("g p n -> p g n").bitcast(I32),
-        )
-        load_x_codes(0)
+
+        def load_x0_passes(g0, g1):
+            nc.sync.dma_start(
+                out=xr_codes[0][:, g0:g1, :].bitcast(I32),
+                in_=x_words[g0:g1, :, : 2 * CHUNK].rearrange("g p n -> p g n").bitcast(I32),
+            )
+
+        def load_first_w_passes(g0, g1):
+            nc.sync.dma_start(
+                out=w_codes[first_k][:, g0:g1, :].bitcast(I32),
+                in_=Wqkv_words[g0:g1, :, 2 * BANK * first_k : 2 * BANK * (first_k + 1)].rearrange("g p n -> p g n").bitcast(I32),
+            )
+
+        x0_scales = x_scales[:, :, :CHUNK]
+        w0_scales = Wqkv_scales[:, :, BANK * first_k : BANK * (first_k + 1)]
+        for q in range(3):
+            load_scale_quadrant(xr_planes[0], x0_scales, q)
+        load_x0_passes(0, 1)
+        load_first_w_passes(0, 1)
+        load_scale_quadrant(xr_planes[0], x0_scales, 3)
+        load_scale_rows(w_planes[first_k], w0_scales)
+        load_x0_passes(1, G)
+        load_first_w_passes(1, 2)
+        load_first_w_passes(2, G)
         for kind, n in loads[2:]:
             if kind == "x":
                 load_x_scales(n)
@@ -254,6 +266,22 @@ def tile_attention_pa_kernel(
             if part < 2:
                 t1 = prod.tile([P, TOK, BANK], F32, name="t1", tag="t1", align_bytes=64)
                 t2 = prod.tile([P, TOK, BANK], F32, name="t2", tag="t2", align_bytes=64)
+            first_accs = []
+            if job == 0:
+                for t in range(TOK):
+                    first_acc = psum.tile([P, BANK], F32, name="bank%d" % bank_of(job, t), tag="bank%d" % bank_of(job, t))
+                    first_accs.append(first_acc)
+                for g in range(G):
+                    for t in range(TOK):
+                        nc.tensor.matmul_mx(
+                            out=first_accs[t][:],
+                            lhsT=xr_codes[0][:, g, 2 * P * t : 2 * P * (t + 1)].bitcast(FP4X4),
+                            lhsT_scale=xr_planes[0][:, g, P * t : P * (t + 1)],
+                            rhs=w_codes[k][:, g, :].bitcast(FP4X4),
+                            rhs_scale=w_planes[k][:, g, :],
+                            start=(g == 0),
+                            stop=(g == G - 1),
+                        )
             for t in range(TOK):
                 if job == len(order) - 1 and t == TOK - 1:
                     windows = [
@@ -263,12 +291,12 @@ def tile_attention_pa_kernel(
                 else:
                     windows = [(0, BANK, bank_of(job, t))]
                 for w, (a0, width, bank) in enumerate(windows):
-                    acc = psum.tile([P, width], F32, name="bank%d" % bank, tag="bank%d" % bank)
-                    for g in range(G):
-                        if job == 0 and t == 0:
-                            lhsT = by_pass(x_first[:])[:, g, :]
-                            lhsT_scale = xr_planes[0][:, g, :P]
-                        elif natural:
+                    if job == 0:
+                        acc = first_accs[t]
+                    else:
+                        acc = psum.tile([P, width], F32, name="bank%d" % bank, tag="bank%d" % bank)
+                    for g in range(G if job > 0 else 0):
+                        if natural:
                             lhsT = xr_codes[0][:, g, 2 * P * t : 2 * P * (t + 1)]
                             lhsT_scale = xr_planes[0][:, g, P * t : P * (t + 1)]
                         else:

@@ -28,6 +28,7 @@ FIRST_HEAD = [0, 5, 10, 16]
 RAW_CODES = G * 2 * CHUNK
 SPINS = 8
 LAST_N = 512
+LAST_WINDOWS = [(0, 256), (256, 128), (384, 128)]
 HEAD_JOBS = 4
 TAIL_JOBS = 5
 
@@ -266,6 +267,36 @@ def tile_attention_pa_kernel(
             if part < 2:
                 t1 = prod.tile([P, TOK, BANK], F32, name="t1", tag="t1", align_bytes=64)
                 t2 = prod.tile([P, TOK, BANK], F32, name="t2", tag="t2", align_bytes=64)
+            if job == len(order) - 1:
+                for w, (a0, width) in enumerate(LAST_WINDOWS):
+                    for t in range(TOK):
+                        bank = bank_of(job - w % 2, t)
+                        acc = psum.tile([P, width], F32, name="bank%d" % bank, tag="bank%d" % bank)
+                        for g in range(G):
+                            nc.tensor.matmul_mx(
+                                out=acc[:],
+                                lhsT=x_tiles[c][t][0][:, g, :].bitcast(FP4X4),
+                                lhsT_scale=x_tiles[c][t][1][:, g, :],
+                                rhs=w_codes[k][:, g, 2 * a0 : 2 * (a0 + width)].bitcast(FP4X4),
+                                rhs_scale=w_planes[k][:, g, a0 : a0 + width],
+                                start=(g == 0),
+                                stop=(g == G - 1),
+                            )
+                        copy_out = nc.vector.tensor_copy if t % 2 == 0 else nc.scalar.copy
+                        for a, n, head, d in pieces(BANK * i + a0, width):
+                            if n > DH:
+                                copy_out(
+                                    out=stage_view(c, part, head, n // DH)[:, :, t, :],
+                                    in_=acc[:, a : a + n].rearrange("p (h d) -> p h d", d=DH),
+                                )
+                            else:
+                                copy_out(out=stage_view(c, part, head, 1)[:, 0, t, d : d + n], in_=acc[:, a : a + n])
+                    h0, h1 = (BANK * i + a0) // DH - FIRST_HEAD[i], (BANK * i + a0 + width) // DH - FIRST_HEAD[i]
+                    nc.sync.dma_start(
+                        out=dst.rearrange("h (p t) d -> p h (t d)", t=TOK)[:, h0:h1, :],
+                        in_=stage[(c, part, i)][:, h0:h1].rearrange("p h t d -> p h (t d)"),
+                    )
+                continue
             first_accs = []
             if job == 0:
                 for t in range(TOK):

@@ -29,6 +29,8 @@ RAW_CODES = G * 2 * CHUNK
 SPINS = 8
 LAST_N = 512
 LAST_WINDOWS = [(0, 256), (256, 128), (384, 128)]
+TAIL_WINDOWS = [(0, 256), (256, 256)]
+WINDOW_JOBS = 4
 HEAD_JOBS = 4
 TAIL_JOBS = 5
 
@@ -267,10 +269,12 @@ def tile_attention_pa_kernel(
             if part < 2:
                 t1 = prod.tile([P, TOK, BANK], F32, name="t1", tag="t1", align_bytes=64)
                 t2 = prod.tile([P, TOK, BANK], F32, name="t2", tag="t2", align_bytes=64)
-            if job == len(order) - 1:
-                for w, (a0, width) in enumerate(LAST_WINDOWS):
+            if job >= len(order) - WINDOW_JOBS:
+                last = job == len(order) - 1
+                job_windows = LAST_WINDOWS if last else TAIL_WINDOWS
+                for w, (a0, width) in enumerate(job_windows):
                     for t in range(TOK):
-                        bank = bank_of(job - w % 2, t)
+                        bank = bank_of(len(order) - WINDOW_JOBS - w % 2, t)
                         acc = psum.tile([P, width], F32, name="bank%d" % bank, tag="bank%d" % bank)
                         for g in range(G):
                             nc.tensor.matmul_mx(
@@ -282,7 +286,7 @@ def tile_attention_pa_kernel(
                                 start=(g == 0),
                                 stop=(g == G - 1),
                             )
-                        copy_out = nc.vector.tensor_copy if t % 2 == 0 else nc.scalar.copy
+                        copy_out = nc.vector.tensor_copy if last and t % 2 == 0 else nc.scalar.copy
                         for a, n, head, d in pieces(BANK * i + a0, width):
                             if n > DH:
                                 copy_out(
@@ -291,11 +295,16 @@ def tile_attention_pa_kernel(
                                 )
                             else:
                                 copy_out(out=stage_view(c, part, head, 1)[:, 0, t, d : d + n], in_=acc[:, a : a + n])
-                    h0, h1 = (BANK * i + a0) // DH - FIRST_HEAD[i], (BANK * i + a0 + width) // DH - FIRST_HEAD[i]
-                    nc.sync.dma_start(
-                        out=dst.rearrange("h (p t) d -> p h (t d)", t=TOK)[:, h0:h1, :],
-                        in_=stage[(c, part, i)][:, h0:h1].rearrange("p h t d -> p h (t d)"),
-                    )
+                        h0, h1 = (BANK * i + a0) // DH - FIRST_HEAD[i], (BANK * i + a0 + width) // DH - FIRST_HEAD[i]
+                        group = TOK
+                        store_queue = nc.sync if last else nc.scalar
+                        if (t + 1) % group == 0:
+                            store_queue.dma_start(
+                                out=dst.rearrange("h (p t) d -> p h t d", t=TOK)[:, h0:h1, t + 1 - group : t + 1, :].rearrange(
+                                    "p h t d -> p h (t d)"
+                                ),
+                                in_=stage[(c, part, i)][:, h0:h1, t + 1 - group : t + 1, :].rearrange("p h t d -> p h (t d)"),
+                            )
                 continue
             first_accs = []
             if job == 0:

@@ -286,7 +286,7 @@ def tile_attention_pa_kernel(
                                 start=(g == 0),
                                 stop=(g == G - 1),
                             )
-                        copy_out = nc.vector.tensor_copy if last and t % 2 == 0 else nc.scalar.copy
+                        copy_out = nc.scalar.copy
                         for a, n, head, d in pieces(BANK * i + a0, width):
                             if n > DH:
                                 copy_out(
@@ -297,7 +297,7 @@ def tile_attention_pa_kernel(
                                 copy_out(out=stage_view(c, part, head, 1)[:, 0, t, d : d + n], in_=acc[:, a : a + n])
                         h0, h1 = (BANK * i + a0) // DH - FIRST_HEAD[i], (BANK * i + a0 + width) // DH - FIRST_HEAD[i]
                         group = TOK
-                        store_queue = nc.sync if last else nc.scalar
+                        store_queue = nc.scalar
                         if (t + 1) % group == 0:
                             store_queue.dma_start(
                                 out=dst.rearrange("h (p t) d -> p h t d", t=TOK)[:, h0:h1, t + 1 - group : t + 1, :].rearrange(

@@ -56,6 +56,14 @@ def tile_attention_pa_kernel(
 
         w_code_tiles = [keep.tile([P, G * 2 * BANK], U8, name="w_codes%d" % k, align_bytes=64) for k in range(3 * NB)]
         w_plane_tiles = [keep.tile([P, G * BANK], U8, name="w_planes%d" % k, align_bytes=64) for k in range(3 * NB)]
+        xc_tiles = {}
+        xs_tiles = {}
+        for c in range(NCHUNK):
+            for t in range(TOK):
+                xc_tiles[(c, t)] = keep.tile([P, G * 2 * P], U8, name="xc%d_%d" % (c, t), align_bytes=64)
+        for c in range(NCHUNK):
+            for t in range(TOK):
+                xs_tiles[(c, t)] = keep.tile([P, G * P], U8, name="xs%d_%d" % (c, t), align_bytes=64)
         w_codes = [by_pass(tile_[:]) for tile_ in w_code_tiles]
         w_planes = [by_pass(tile_[:]) for tile_ in w_plane_tiles]
         raw = [
@@ -100,12 +108,12 @@ def tile_attention_pa_kernel(
             nc.vector.memset(w_plane_tiles[k][:].bitcast(I32), 0)
 
         def permute(c, t):
-            xc = keep.tile([P, G * 2 * P], U8, name="xc%d_%d" % (c, t), align_bytes=64)
+            xc = xc_tiles[(c, t)]
             nc.vector.tensor_copy(
                 out=by_pass(xc[:]).rearrange("p g (m b) -> p g m b", b=2),
                 in_=xr_codes[c].rearrange("p g (m t b) -> p t g m b", t=TOK, b=2)[:, t],
             )
-            xs = keep.tile([P, G * P], U8, name="xs%d_%d" % (c, t), align_bytes=64)
+            xs = xs_tiles[(c, t)]
             nc.vector.tensor_copy(out=by_pass(xs[:]), in_=xr_planes[c].rearrange("p g (m t) -> p t g m", t=TOK)[:, t])
             return by_pass(xc[:]), by_pass(xs[:])
 

from contextlib import ExitStack

import concourse.mybir as mybir

F32 = mybir.dt.float32
BF16 = mybir.dt.bfloat16
U8 = mybir.dt.uint8
I32 = mybir.dt.int32
FP4X4 = mybir.dt.float4_e2m1fn_x4
ACT = mybir.ActivationFunctionType
ALU = mybir.AluOpType

P = 128
G = 4
TOK = 4
CHUNK = P * TOK
NCHUNK = 4
HEADS = 16
DH = 96
PART = HEADS * DH
BANK = 512
NB = PART // BANK
GRP = 32
HALF = GRP // 2
REP = 6
TABW = REP * DH
FIRST_HEAD = [0, 5, 10, 16]
RAW_CODES = G * 2 * CHUNK
SPINS = 8
LAST_N = 512
LAST_WINDOWS = [(0, 256), (256, 128), (384, 128)]
TAIL_WINDOWS = [(0, 256), (256, 256)]
WINDOW_JOBS = 4
HEAD_JOBS = 4
TAIL_JOBS = 5

FLOPS = 2 * 2048 * 2048 * 4608


def tile_attention_pa_kernel(
    tc, x_words, x_scales, f1, f2, f3, Wqkv_words, Wqkv_scales, out_0, out_1, out_2
):
    nc = tc.nc
    outs = (out_0, out_1, out_2)

    with ExitStack() as ctx:
        keep = ctx.enter_context(tc.tile_pool(name="keep", bufs=1))
        prod = ctx.enter_context(tc.tile_pool(name="prod", bufs=3))
        stages = ctx.enter_context(tc.tile_pool(name="stages", bufs=2))
        vstages = ctx.enter_context(tc.tile_pool(name="vstages", bufs=1))
        psum = ctx.enter_context(tc.psum_pool(name="psum", bufs=1))
        ctx.enter_context(tc.manual_schedule())

        def by_pass(flat):
            return flat.rearrange("p (g n) -> p g n", g=G)

        w_code_tiles = [keep.tile([P, G * 2 * BANK], U8, name="w_codes%d" % k, align_bytes=64) for k in range(3 * NB)]
        w_plane_tiles = [keep.tile([P, G * BANK], U8, name="w_planes%d" % k, align_bytes=64) for k in range(3 * NB)]
        xc_tiles = {}
        xs_tiles = {}
        for c in range(NCHUNK):
            for t in range(TOK):
                xc_tiles[(c, t)] = keep.tile([P, G * 2 * P], U8, name="xc%d_%d" % (c, t), align_bytes=64)
        for c in range(NCHUNK):
            for t in range(TOK):
                xs_tiles[(c, t)] = keep.tile([P, G * P], U8, name="xs%d_%d" % (c, t), align_bytes=64)
        w_codes = [by_pass(tile_[:]) for tile_ in w_code_tiles]
        w_planes = [by_pass(tile_[:]) for tile_ in w_plane_tiles]
        raw = [
            prod.tile([P, RAW_CODES + G * CHUNK], U8, name="raw%d" % c, tag="t%d" % (1 + c % 2), align_bytes=64)
            for c in range(NCHUNK)
        ]
        xr_codes = [by_pass(tile_[:, :RAW_CODES]) for tile_ in raw]
        xr_planes = [by_pass(tile_[:, RAW_CODES:]) for tile_ in raw]

        def load_scale_quadrant(planes, scales, q):
            nc.sync.dma_start(
                out=planes[32 * q : 32 * q + 4, :, :].bitcast(I32),
                in_=scales[:, 4 * q : 4 * q + 4, :].rearrange("g r n -> r g n").bitcast(I32),
            )

        def load_scale_rows(planes, scales):
            for q in range(4):
                load_scale_quadrant(planes, scales, q)

        def load_x_codes(c):
            nc.sync.dma_start(
                out=xr_codes[c].bitcast(I32),
                in_=x_words[:, :, 2 * CHUNK * c : 2 * CHUNK * (c + 1)].rearrange("g p n -> p g n").bitcast(I32),
            )

        def load_x_scales(c):
            load_scale_rows(xr_planes[c], x_scales[:, :, CHUNK * c : CHUNK * (c + 1)])

        def load_w_codes(k):
            nc.sync.dma_start(
                out=w_codes[k].bitcast(I32),
                in_=Wqkv_words[:, :, 2 * BANK * k : 2 * BANK * (k + 1)].rearrange("g p n -> p g n").bitcast(I32),
            )

        def load_w_scales(k):
            load_scale_rows(w_planes[k], Wqkv_scales[:, :, BANK * k : BANK * (k + 1)])

        def zero_x_planes(c):
            nc.vector.memset(raw[c][:, RAW_CODES:].bitcast(I32), 0)

        def zero_w_planes(k):
            nc.vector.memset(w_plane_tiles[k][:].bitcast(I32), 0)

        def permute(c, t):
            xc = xc_tiles[(c, t)]
            nc.vector.tensor_copy(
                out=by_pass(xc[:]).rearrange("p g (m b) -> p g m b", b=2),
                in_=xr_codes[c].rearrange("p g (m t b) -> p t g m b", t=TOK, b=2)[:, t],
            )
            xs = xs_tiles[(c, t)]
            nc.vector.tensor_copy(out=by_pass(xs[:]), in_=xr_planes[c].rearrange("p g (m t) -> p t g m", t=TOK)[:, t])
            return by_pass(xc[:]), by_pass(xs[:])

        rope_jobs = [(c, part, i) for c in range(NCHUNK) for part in (0, 1) for i in range(NB)]
        value_jobs = [(c, 2, i) for c in range(NCHUNK) for i in range(NB)]
        woven = value_jobs[HEAD_JOBS:-TAIL_JOBS]
        order = value_jobs[:HEAD_JOBS]
        placed = 0
        for r, rope_job in enumerate(rope_jobs):
            order.append(rope_job)
            if placed < len(woven) and (r + 1) * (len(woven) + 1) >= (placed + 1) * len(rope_jobs):
                order.append(woven[placed])
                placed += 1
        order.extend(value_jobs[-TAIL_JOBS:])

        warm = keep.tile([P, 1], F32, name="warm")
        warm2 = keep.tile([P, 1], F32, name="warm2")
        nc.gpsimd.memset(warm[:], 0.0)
        idle = keep.tile([P, BANK], BF16, name="idle")
        nc.gpsimd.memset(idle[:], 0.0)
        spin = psum.tile([P, BANK], F32, name="bank7", tag="bank7")
        for n in range(SPINS):
            nc.tensor.matmul(out=spin[:], lhsT=idle[:, :P], rhs=idle[:], start=True, stop=True)
        fraw = keep.tile([P, 3, 2, TOK, GRP], BF16, name="fraw")
        for i, f in enumerate((f1, f2, f3)):
            nc.scalar.dma_start(
                out=fraw[:, i].rearrange("p c t j -> p c (t j)"),
                in_=f.rearrange("(c p t) j -> p c (t j)", c=2, t=TOK),
            )
        nc.scalar.activation(out=warm2[:], in_=warm[:], func=ACT.Sin)

        strips = []
        for c, part, i in order:
            if NB * part + i not in strips:
                strips.append(NB * part + i)
        loads = [("x", 0), ("w", strips[0]), ("w", strips[1]), ("x", 1), ("w", strips[2]), ("x", 2), ("x", 3)]
        for kind, n in loads:
            if kind == "x":
                zero_x_planes(n)
            else:
                zero_w_planes(n)
        first_k = strips[0]

        def load_x0_passes(g0, g1):
            nc.sync.dma_start(
                out=xr_codes[0][:, g0:g1, :].bitcast(I32),
                in_=x_words[g0:g1, :, : 2 * CHUNK].rearrange("g p n -> p g n").bitcast(I32),
            )

        def load_first_w_passes(g0, g1):
            nc.sync.dma_start(
                out=w_codes[first_k][:, g0:g1, :].bitcast(I32),
                in_=Wqkv_words[g0:g1, :, 2 * BANK * first_k : 2 * BANK * (first_k + 1)].rearrange("g p n -> p g n").bitcast(I32),
            )

        x0_scales = x_scales[:, :, :CHUNK]
        w0_scales = Wqkv_scales[:, :, BANK * first_k : BANK * (first_k + 1)]
        for q in range(3):
            load_scale_quadrant(xr_planes[0], x0_scales, q)
        load_x0_passes(0, 1)
        load_first_w_passes(0, 1)
        load_scale_quadrant(xr_planes[0], x0_scales, 3)
        load_scale_rows(w_planes[first_k], w0_scales)
        load_x0_passes(1, G)
        load_first_w_passes(1, 2)
        load_first_w_passes(2, G)
        for kind, n in loads[2:]:
            if kind == "x":
                load_x_scales(n)
                load_x_codes(n)
            else:
                load_w_scales(n)
                load_w_codes(n)

        half = stages.tile([P, 3, 2, TOK, GRP], F32, name="half", tag="stage0")
        sq = stages.tile([P, 3, 2, TOK, GRP], F32, name="sq", tag="stage1")
        nc.scalar.activation(
            out=half[:].rearrange("p i c t j -> p (i c t j)"),
            in_=fraw[:].rearrange("p i c t j -> p (i c t j)"),
            func=ACT.Sin,
            scale=0.5,
        )
        nc.scalar.activation(
            out=sq[:].rearrange("p i c t j -> p (i c t j)"),
            in_=half[:].rearrange("p i c t j -> p (i c t j)"),
            func=ACT.Square,
        )
        cos_tab = {}
        sin_tab = {}

        def build_tables(cc, t):
            ct = keep.tile([P, TABW], F32, name="cos%d_%d" % (cc, t))
            nc.scalar.activation(
                out=ct[:].rearrange("p (r i j) -> p r i j", i=3, j=GRP),
                in_=sq[:, :, cc, t, :].unsqueeze(1).to_broadcast([P, REP, 3, GRP]),
                func=ACT.Copy,
                scale=-2.0,
                bias=1.0,
            )
            st = keep.tile([P, TABW], F32, name="sin%d_%d" % (cc, t))
            sv = st[:].rearrange("p (r i h j) -> p r i h j", i=3, h=2, j=HALF)
            for h, sign in ((0, -1.0), (1, 1.0)):
                nc.scalar.activation(
                    out=sv[:, :, :, h, :],
                    in_=fraw[:, :, cc, t, HALF * h : HALF * (h + 1)].unsqueeze(1).to_broadcast([P, REP, 3, HALF]),
                    func=ACT.Sin,
                    scale=sign,
                )
            cos_tab[(cc, t)] = ct
            sin_tab[(cc, t)] = st

        for t in range(TOK):
            build_tables(0, t)

        x_tiles = {}
        x_tiles[1] = [permute(1, t) for t in range(TOK)]
        for k in strips[3:]:
            zero_w_planes(k)
        for k in strips[3:]:
            load_w_scales(k)
            load_w_codes(k)
        for c in (0, 2, 3):
            x_tiles[c] = [permute(c, t) for t in range(TOK)]

        def pieces(c0, width):
            lead = min((-c0) % DH, width)
            whole = (width - lead) // DH
            tail = width - lead - whole * DH
            runs = []
            if lead:
                runs.append((0, lead, c0 // DH, c0 % DH))
            if whole:
                runs.append((lead, whole * DH, (c0 + lead) // DH, 0))
            if tail:
                runs.append((width - tail, tail, (c0 + lead) // DH + whole, 0))
            return runs

        def bank_of(job, t):
            pair = 2 * job + t // 2
            return 2 * (pair % 4) + (t + pair // 4) % 2

        stage = {}

        def stage_view(c, part, head, n_heads):
            j = max(k for k in range(NB) if FIRST_HEAD[k] <= head)
            return stage[(c, part, j)][:, head - FIRST_HEAD[j] : head - FIRST_HEAD[j] + n_heads]

        for job, (c, part, i) in enumerate(order):
            b, cc = divmod(c, 2)
            natural = c == 0 and part == 2
            by_token = natural or job == len(order) - 1
            pool, prefix = (vstages, "vstage") if part == 2 and not natural else (stages, "stage")
            for j in range(i, min(i + 2, NB)):
                if (c, part, j) not in stage:
                    stage[(c, part, j)] = pool.tile(
                        [P, FIRST_HEAD[j + 1] - FIRST_HEAD[j], TOK, DH], F32, name="%s%d" % (prefix, j), tag="%s%d" % (prefix, j)
                    )
            dst = outs[part][b, FIRST_HEAD[i] : FIRST_HEAD[i + 1], CHUNK * cc : CHUNK * (cc + 1), :]
            eng = nc.sync if part < 2 else nc.scalar
            k = NB * part + i
            if part < 2:
                t1 = prod.tile([P, TOK, BANK], F32, name="t1", tag="t1", align_bytes=64)
                t2 = prod.tile([P, TOK, BANK], F32, name="t2", tag="t2", align_bytes=64)
            if job >= len(order) - WINDOW_JOBS:
                last = job == len(order) - 1
                job_windows = LAST_WINDOWS if last else TAIL_WINDOWS
                for w, (a0, width) in enumerate(job_windows):
                    for t in range(TOK):
                        bank = bank_of(len(order) - WINDOW_JOBS - w % 2, t)
                        acc = psum.tile([P, width], F32, name="bank%d" % bank, tag="bank%d" % bank)
                        for g in range(G):
                            nc.tensor.matmul_mx(
                                out=acc[:],
                                lhsT=x_tiles[c][t][0][:, g, :].bitcast(FP4X4),
                                lhsT_scale=x_tiles[c][t][1][:, g, :],
                                rhs=w_codes[k][:, g, 2 * a0 : 2 * (a0 + width)].bitcast(FP4X4),
                                rhs_scale=w_planes[k][:, g, a0 : a0 + width],
                                start=(g == 0),
                                stop=(g == G - 1),
                            )
                        copy_out = nc.scalar.copy
                        for a, n, head, d in pieces(BANK * i + a0, width):
                            if n > DH:
                                copy_out(
                                    out=stage_view(c, part, head, n // DH)[:, :, t, :],
                                    in_=acc[:, a : a + n].rearrange("p (h d) -> p h d", d=DH),
                                )
                            else:
                                copy_out(out=stage_view(c, part, head, 1)[:, 0, t, d : d + n], in_=acc[:, a : a + n])
                        h0, h1 = (BANK * i + a0) // DH - FIRST_HEAD[i], (BANK * i + a0 + width) // DH - FIRST_HEAD[i]
                        group = TOK
                        store_queue = nc.scalar
                        if (t + 1) % group == 0:
                            store_queue.dma_start(
                                out=dst.rearrange("h (p t) d -> p h t d", t=TOK)[:, h0:h1, t + 1 - group : t + 1, :].rearrange(
                                    "p h t d -> p h (t d)"
                                ),
                                in_=stage[(c, part, i)][:, h0:h1, t + 1 - group : t + 1, :].rearrange("p h t d -> p h (t d)"),
                            )
                continue
            first_accs = []
            if job == 0:
                for t in range(TOK):
                    first_acc = psum.tile([P, BANK], F32, name="bank%d" % bank_of(job, t), tag="bank%d" % bank_of(job, t))
                    first_accs.append(first_acc)
                for g in range(G):
                    for t in range(TOK):
                        nc.tensor.matmul_mx(
                            out=first_accs[t][:],
                            lhsT=xr_codes[0][:, g, 2 * P * t : 2 * P * (t + 1)].bitcast(FP4X4),
                            lhsT_scale=xr_planes[0][:, g, P * t : P * (t + 1)],
                            rhs=w_codes[k][:, g, :].bitcast(FP4X4),
                            rhs_scale=w_planes[k][:, g, :],
                            start=(g == 0),
                            stop=(g == G - 1),
                        )
            for t in range(TOK):
                if job == len(order) - 1 and t == TOK - 1:
                    windows = [
                        (LAST_N * n, LAST_N, bank_of(job, t) if n == 0 else bank_of(job - 1, n - 1))
                        for n in range(BANK // LAST_N)
                    ]
                else:
                    windows = [(0, BANK, bank_of(job, t))]
                for w, (a0, width, bank) in enumerate(windows):
                    if job == 0:
                        acc = first_accs[t]
                    else:
                        acc = psum.tile([P, width], F32, name="bank%d" % bank, tag="bank%d" % bank)
                    for g in range(G if job > 0 else 0):
                        if natural:
                            lhsT = xr_codes[0][:, g, 2 * P * t : 2 * P * (t + 1)]
                            lhsT_scale = xr_planes[0][:, g, P * t : P * (t + 1)]
                        else:
                            lhsT = x_tiles[c][t][0][:, g, :]
                            lhsT_scale = x_tiles[c][t][1][:, g, :]
                        nc.tensor.matmul_mx(
                            out=acc[:],
                            lhsT=lhsT.bitcast(FP4X4),
                            lhsT_scale=lhsT_scale,
                            rhs=w_codes[k][:, g, 2 * a0 : 2 * (a0 + width)].bitcast(FP4X4),
                            rhs_scale=w_planes[k][:, g, a0 : a0 + width],
                            start=(g == 0),
                            stop=(g == G - 1),
                        )
                    if part < 2:
                        tab = slice(GRP * i, GRP * i + BANK)
                        nc.vector.tensor_tensor(out=t1[:, t, :], in0=acc[:], in1=cos_tab[(cc, t)][:, tab], op=ALU.mult)
                        u = acc[:].rearrange("p (a h j) -> p a h j", h=2, j=HALF)
                        t2v = t2[:, t, :].rearrange("p (a h j) -> p a h j", h=2, j=HALF)
                        sv = sin_tab[(cc, t)][:, tab].rearrange("p (a h j) -> p a h j", h=2, j=HALF)
                        nc.vector.tensor_tensor(out=t2v, in0=u[:, :, ::-1, :], in1=sv, op=ALU.mult)
                        continue
                    by_vector = len(windows) > 1 and w % 2 == 0
                    copy_out = nc.vector.tensor_copy if by_vector else nc.scalar.copy
                    for a, n, head, d in pieces(BANK * i + a0, width):
                        if n > DH:
                            copy_out(
                                out=stage_view(c, part, head, n // DH)[:, :, t, :],
                                in_=acc[:, a : a + n].rearrange("p (h d) -> p h d", d=DH),
                            )
                        else:
                            copy_out(out=stage_view(c, part, head, 1)[:, 0, t, d : d + n], in_=acc[:, a : a + n])
                    h0, h1 = (BANK * i + a0) // DH - FIRST_HEAD[i], (BANK * i + a0 + width) // DH - FIRST_HEAD[i]
                    if natural:
                        nc.sync.dma_start(
                            out=dst[:, P * t : P * (t + 1), :].rearrange("h p d -> p h d"),
                            in_=stage[(c, part, i)][:, :, t, :],
                        )
                    elif by_token and t % 2 == 1:
                        nc.scalar.dma_start(
                            out=dst.rearrange("h (p t) d -> p h t d", t=TOK)[:, :, t - 1 : t + 1, :].rearrange("p h t d -> p h (t d)"),
                            in_=stage[(c, part, i)][:, :, t - 1 : t + 1, :].rearrange("p h t d -> p h (t d)"),
                        )
            if job == HEAD_JOBS - 1:
                for t in range(TOK):
                    build_tables(1, t)
            if part < 2:
                adder = nc.vector if (c, part, i) == rope_jobs[-1] else nc.gpsimd
                for a, n, head, d in pieces(BANK * i, BANK):
                    if n > DH:
                        adder.tensor_tensor(
                            out=stage_view(c, part, head, n // DH),
                            in0=t1[:, :, a : a + n].rearrange("p t (h d) -> p h t d", d=DH),
                            in1=t2[:, :, a : a + n].rearrange("p t (h d) -> p h t d", d=DH),
                            op=ALU.add,
                        )
                    else:
                        adder.tensor_tensor(
                            out=stage_view(c, part, head, 1)[:, 0, :, d : d + n],
                            in0=t1[:, :, a : a + n],
                            in1=t2[:, :, a : a + n],
                            op=ALU.add,
                        )
            if not by_token:
                eng.dma_start(
                    out=dst.rearrange("h (p t) d -> p h (t d)", t=TOK),
                    in_=stage[(c, part, i)][:].rearrange("p h t d -> p h (t d)"),
                )
